import numpy as np
import ml_dtypes


def mxq(x, axis, fmt="e4m3"):
    dtype, down = {"e4m3": (ml_dtypes.float8_e4m3fn, 7), "e5m2": (ml_dtypes.float8_e5m2, 14)}[fmt]
    v = np.moveaxis(np.asarray(x, np.float32).astype(ml_dtypes.bfloat16).astype(np.float64), axis, -1)
    blocks = v.reshape(v.shape[:-1] + (-1, 32))
    amax = np.abs(blocks).max(-1, keepdims=True)
    byte = np.maximum(np.where(amax > 0, np.frexp(amax)[1] - 1 + 127, 0) - down, 1)
    scale = np.exp2(byte - 127.0)
    codes = (blocks / scale).astype(np.float32).astype(dtype).astype(np.float64)
    return np.moveaxis((codes * scale).reshape(v.shape), -1, axis)


WIDE = False


def mx_kscale(k):
    if not WIDE:
        return np.ones(k)
    levels = np.array([10, -10, 5, -5, 0])
    a = np.random.permutation(np.resize(levels, k // 512 * 4)).reshape(k // 512, 4)
    idx = np.arange(k)
    return np.exp2(a[idx // 512, idx % 128 // 32])


BF16 = ml_dtypes.bfloat16


def bf(x):
    return np.asarray(x, np.float32).astype(BF16)


def f64(x):
    return np.asarray(x).astype(np.float64)


B, C, P, D = 2, 512, 128, 512
EPS = 1e-5


def layer_norm(v, w, b):
    m = v.mean(-1, keepdims=True)
    var = ((v - m) ** 2).mean(-1, keepdims=True)
    return (v - m) * (1.0 / np.sqrt(var + EPS)) * w + b


def setup_inputs():
    s = mx_kscale(2 * D)
    return {"prev_cell_out": bf(np.random.standard_normal((B, P, D)) * s[D:]),
            "emb_prompt": bf(np.random.standard_normal((P, D)) / np.sqrt(D)),
            "ln_prompt_w": bf((1.0 + 0.1 * np.random.standard_normal(D)) * s[:D]),
            "ln_prompt_b": bf(0.1 * np.random.standard_normal(D) * s[:D]),
            "W_imp": bf(np.random.standard_normal((2 * D, D)) / D / s[:, None]),
            "b_imp": bf(np.random.standard_normal(D) / np.sqrt(D)),
            "emb_column": bf(0.01 * np.random.standard_normal((C, D))),
            "ln_col_w": bf(1.0 + 0.1 * np.random.standard_normal(D)),
            "ln_col_b": bf(0.1 * np.random.standard_normal(D))}


def reference(prev_cell_out, emb_prompt, ln_prompt_w, ln_prompt_b, W_imp, b_imp, emb_column, ln_col_w, ln_col_b):
    p0 = f64(emb_prompt)
    w = f64(W_imp)
    pn = layer_norm(p0, f64(ln_prompt_w), f64(ln_prompt_b))
    from_prompt = mxq(pn, 1, "e4m3") @ mxq(w[:D], 0, "e4m3")
    from_prev = mxq(f64(prev_cell_out), 2, "e4m3") @ mxq(w[D:], 0, "e4m3")
    x_prompt = from_prompt[None] + from_prev + f64(b_imp) + p0[None]
    col_t = layer_norm(f64(emb_column), f64(ln_col_w), f64(ln_col_b)).T
    return mxq(x_prompt, 2, "e4m3") @ mxq(col_t, 0, "e4m3")

@@ -1,0 +1,308 @@
+from contextlib import ExitStack
+
+import concourse.mybir as mybir
+from concourse.masks import make_identity
+
+F32 = mybir.dt.float32
+BF16 = mybir.dt.bfloat16
+U32 = mybir.dt.uint32
+U8 = mybir.dt.uint8
+FP8X4 = mybir.dt.float8_e4m3fn_x4
+ALU = mybir.AluOpType
+ACT = mybir.ActivationFunctionType
+
+P = 128
+PACK = 4
+D = P * PACK
+SAMPLES = 2
+COLUMNS = 512
+COLUMN_TILES = COLUMNS // P
+ROW_TILES = 1 + COLUMN_TILES
+EPS = 1e-5
+RUN = 4
+SCALAR_BANKS = 3
+
+FLOPS = 2 * P * D * D + 2 * SAMPLES * P * D * D + 2 * SAMPLES * P * D * COLUMNS
+
+LN_PROMPT_W = 0
+LN_PROMPT_B = 1
+B_IMP = 2
+LN_COL_W = 3
+LN_COL_B = 4
+VECTORS = 5
+
+
+def group_words(copy, grouped, planes):
+    copy(
+        out=grouped.rearrange("p (c i) t -> p c t i", i=RUN),
+        in_=planes.rearrange("p t (c i) -> p c t i", i=RUN),
+    )
+
+
+def quantise(nc, codes, scales, grouped):
+    nc.vector.quantize_mx(
+        out=codes.bitcast(FP8X4),
+        scales=scales,
+        in_=grouped.rearrange("p c t -> p (c t)"),
+    )
+
+
+def tile_tromptcell_pa_s_kernel(
+    tc,
+    prev_cell_out,
+    emb_prompt,
+    ln_prompt_w,
+    ln_prompt_b,
+    W_imp,
+    b_imp,
+    emb_column,
+    ln_col_w,
+    ln_col_b,
+    out,
+):
+    nc = tc.nc
+    with ExitStack() as ctx:
+        keep = ctx.enter_context(tc.tile_pool(name="keep", bufs=1))
+        banks = ctx.enter_context(tc.psum_pool(name="banks", bufs=8))
+        ctx.enter_context(tc.manual_schedule())
+
+        vector_rows = keep.tile([P, P], BF16)
+        vectors = keep.tile([P, VECTORS * PACK], F32)
+        ident_bf16 = keep.tile([P, P], BF16)
+        ident_f32 = keep.tile([P, P], F32)
+        one = keep.tile([P, 1], F32)
+        table_warmer = keep.tile([P, 1], F32)
+
+        prompt_raw = keep.tile([P, D], BF16)
+        column_raw = keep.tile([P, COLUMN_TILES, D], BF16)
+        prev_raw = keep.tile([P, SAMPLES * D], BF16)
+        w_prompt_raw = keep.tile([P, PACK, D], BF16)
+        w_prev_raw = keep.tile([P, PACK, D], BF16)
+
+        stats = keep.tile([P, ROW_TILES, 6], F32)
+        mean_var = keep.tile([P, ROW_TILES, 2], F32)
+        var_eps = keep.tile([P, ROW_TILES], F32)
+        std = keep.tile([P, ROW_TILES], F32)
+        rstd = keep.tile([P, ROW_TILES], F32)
+        z = keep.tile([P, ROW_TILES, D], F32)
+
+        residual = keep.tile([P, PACK, P], F32)
+        pn_planes = keep.tile([P, PACK, P], BF16)
+        col_planes = keep.tile([P, PACK, COLUMNS], BF16)
+
+        def mx_operand(name, columns):
+            grouped = keep.tile([P, columns, PACK], BF16, name=name + "_grouped", align_bytes=64)
+            codes = keep.tile([P, columns], U32, name=name + "_codes", align_bytes=64)
+            scales = keep.tile([P, columns], U8, name=name + "_scales", align_bytes=64)
+            return grouped, codes, scales
+
+        pn_grouped, pn_codes, pn_scales = mx_operand("pn", P)
+        prev_grouped, prev_codes, prev_scales = mx_operand("prev", SAMPLES * P)
+        w_prompt_grouped, w_prompt_codes, w_prompt_scales = mx_operand("w_prompt", D)
+        w_prev_grouped, w_prev_codes, w_prev_scales = mx_operand("w_prev", D)
+        col_grouped, col_codes, col_scales = mx_operand("col", COLUMNS)
+        x_grouped, x_codes, x_scales = zip(*[mx_operand("x%d" % n, P) for n in range(SAMPLES)])
+
+        nc.gpsimd.memset(vector_rows[:], 0.0)
+        for v, vector in enumerate((ln_prompt_w, ln_prompt_b, b_imp, ln_col_w, ln_col_b)):
+            nc.scalar.dma_start(
+                out=vector_rows[PACK * v : PACK * (v + 1), :],
+                in_=vector.rearrange("(t p) -> t p", p=P),
+            )
+        nc.sync.dma_start(out=prompt_raw[:], in_=emb_prompt)
+        column_view = emb_column.rearrange("(ct p) f -> p ct f", p=P)
+        for first in range(0, COLUMN_TILES, 2):
+            nc.sync.dma_start(
+                out=column_raw[:, first : first + 2, :], in_=column_view[:, first : first + 2, :]
+            )
+        nc.sync.dma_start(out=w_prompt_raw[:], in_=W_imp[0:D, :].rearrange("(t p) f -> p t f", p=P))
+        nc.sync.dma_start(
+            out=w_prev_raw[:].rearrange("p (u e) f -> p u e f", u=2),
+            in_=W_imp[D : 2 * D, :].rearrange("(u p e) f -> p u e f", u=2, e=2),
+        )
+        nc.sync.dma_start(
+            out=prev_raw[:].rearrange("p (n f) -> p n f", n=SAMPLES),
+            in_=prev_cell_out.rearrange("n p f -> p n f"),
+        )
+
+        make_identity(nc, ident_bf16[:])
+        make_identity(nc, ident_f32[:])
+        nc.vector.memset(one[:], 1.0)
+        nc.scalar.activation(out=table_warmer[:], in_=one[:], func=ACT.Sqrt)
+
+        row_tiles = [prompt_raw[:]] + [column_raw[:, ct, :] for ct in range(COLUMN_TILES)]
+
+        def statistics(r):
+            nc.vector.bn_stats(out=stats[:, r, :], in_=row_tiles[r])
+            nc.vector.bn_aggr(out=mean_var[:, r, :], in_=stats[:, r, :])
+
+        def standard_deviation(first, last):
+            nc.vector.tensor_scalar_add(
+                out=var_eps[:, first:last], in0=mean_var[:, first:last, 1], scalar1=EPS
+            )
+            nc.scalar.activation(out=std[:, first:last], in_=var_eps[:, first:last], func=ACT.Sqrt)
+
+        def normalise(r):
+            nc.vector.tensor_scalar(
+                out=z[:, r, :],
+                in0=row_tiles[r],
+                scalar1=mean_var[:, r, 0:1],
+                scalar2=rstd[:, r : r + 1],
+                op0=ALU.subtract,
+                op1=ALU.mult,
+            )
+
+        def vector_column(v, t):
+            return vectors[:, PACK * v + t : PACK * v + t + 1]
+
+        statistics(0)
+        standard_deviation(0, 1)
+        prompt_t = banks.tile([P, PACK, P], BF16, tag="bank")
+        for t in range(PACK):
+            nc.tensor.transpose(
+                out=prompt_t[:, t, :], in_=prompt_raw[:, t * P : (t + 1) * P], identity=ident_bf16[:]
+            )
+        statistics(1)
+        nc.vector.reciprocal(out=rstd[:, 0:1], in_=std[:, 0:1])
+        normalise(0)
+
+        vectors_t = banks.tile([P, P], BF16, tag="bank")
+        nc.tensor.transpose(out=vectors_t[:], in_=vector_rows[:], identity=ident_bf16[:])
+        nc.scalar.copy(out=vectors[:], in_=vectors_t[:, 0 : VECTORS * PACK])
+        for t in range(PACK):
+            nc.scalar.activation(
+                out=residual[:, t, :],
+                in_=prompt_t[:, t, :],
+                func=ACT.Identity,
+                bias=vector_column(B_IMP, t),
+            )
+        prompt_z_t = banks.tile([P, PACK, P], F32, tag="bank")
+        for t in range(PACK):
+            nc.tensor.transpose(
+                out=prompt_z_t[:, t, :], in_=z[:, 0, t * P : (t + 1) * P], identity=ident_f32[:]
+            )
+
+        for r in range(2, ROW_TILES):
+            statistics(r)
+        left, right = slice(0, D // 2), slice(D // 2, D)
+        group_words(nc.scalar.copy, w_prev_grouped[:, left, :], w_prev_raw[:, :, left])
+        standard_deviation(1, ROW_TILES)
+        group_words(nc.scalar.copy, w_prev_grouped[:, right, :], w_prev_raw[:, :, right])
+        group_words(nc.vector.tensor_copy, w_prompt_grouped[:, left, :], w_prompt_raw[:, :, left])
+        group_words(nc.vector.tensor_copy, w_prompt_grouped[:, right, :], w_prompt_raw[:, :, right])
+        nc.vector.reciprocal(out=rstd[:, 1:ROW_TILES], in_=std[:, 1:ROW_TILES])
+        for r in range(1, ROW_TILES):
+            normalise(r)
+
+        prev_words = prev_raw[:].bitcast(F32)
+        prev_t = banks.tile([P, SAMPLES * 2, P], F32, tag="bank")
+        for j in range(SAMPLES * 2):
+            nc.tensor.transpose(
+                out=prev_t[:, j, :], in_=prev_words[:, j * P : (j + 1) * P], identity=ident_f32[:]
+            )
+        column_z_t = [
+            banks.tile([P, COLUMNS], F32, tag="bank", name="column_z_t%d" % t) for t in range(PACK)
+        ]
+        for ct in range(COLUMN_TILES):
+            for t in range(PACK):
+                nc.tensor.transpose(
+                    out=column_z_t[t][:, ct * P : (ct + 1) * P],
+                    in_=z[:, 1 + ct, t * P : (t + 1) * P],
+                    identity=ident_f32[:],
+                )
+
+        for t in range(PACK):
+            nc.scalar.activation(
+                out=pn_planes[:, t, :],
+                in_=prompt_z_t[:, t, :],
+                func=ACT.Identity,
+                scale=vector_column(LN_PROMPT_W, t),
+                bias=vector_column(LN_PROMPT_B, t),
+            )
+        nc.vector.tensor_copy(
+            out=prev_grouped[:]
+            .rearrange("p c t -> p (c t)")
+            .bitcast(F32)
+            .rearrange("p (n w u) -> p n w u", n=SAMPLES, u=2),
+            in_=prev_t[:].rearrange("p (n u) w -> p n w u", u=2),
+        )
+        quantise(nc, w_prompt_codes[:], w_prompt_scales[:], w_prompt_grouped[:])
+        group_words(nc.vector.tensor_copy, pn_grouped[:], pn_planes[:])
+        quantise(nc, prev_codes[:], prev_scales[:], prev_grouped[:])
+        quantise(nc, w_prev_codes[:], w_prev_scales[:], w_prev_grouped[:])
+        quantise(nc, pn_codes[:], pn_scales[:], pn_grouped[:])
+
+        for t in range(PACK):
+            if t < SCALAR_BANKS:
+                nc.scalar.activation(
+                    out=col_planes[:, t, :],
+                    in_=column_z_t[t][:],
+                    func=ACT.Identity,
+                    scale=vector_column(LN_COL_W, t),
+                    bias=vector_column(LN_COL_B, t),
+                )
+            else:
+                nc.vector.tensor_scalar(
+                    out=col_planes[:, t, :],
+                    in0=column_z_t[t][:],
+                    scalar1=vector_column(LN_COL_W, t),
+                    scalar2=vector_column(LN_COL_B, t),
+                    op0=ALU.mult,
+                    op1=ALU.add,
+                )
+
+        x_t = [banks.tile([P, PACK, P], F32, tag="bank", name="x_t%d" % n) for n in range(SAMPLES)]
+        for n in range(SAMPLES):
+            prompts = slice(n * P, (n + 1) * P)
+            for t in range(PACK):
+                features = slice(t * P, (t + 1) * P)
+                nc.tensor.matmul_mx(
+                    out=x_t[n][:, t, :],
+                    lhsT=w_prompt_codes[:, features].bitcast(FP8X4),
+                    lhsT_scale=w_prompt_scales[:, features],
+                    rhs=pn_codes[:].bitcast(FP8X4),
+                    rhs_scale=pn_scales[:],
+                    start=True,
+                    stop=False,
+                )
+                nc.tensor.matmul_mx(
+                    out=x_t[n][:, t, :],
+                    lhsT=w_prev_codes[:, features].bitcast(FP8X4),
+                    lhsT_scale=w_prev_scales[:, features],
+                    rhs=prev_codes[:, prompts].bitcast(FP8X4),
+                    rhs_scale=prev_scales[:, prompts],
+                    start=False,
+                    stop=True,
+                )
+
+        def finish_x(n):
+            nc.vector.tensor_tensor(
+                out=x_grouped[n][:],
+                in0=x_t[n][:].rearrange("p t w -> p w t"),
+                in1=residual[:].rearrange("p t w -> p w t"),
+                op=ALU.add,
+            )
+
+        def score(n, copy):
+            scores = banks.tile([P, COLUMNS], F32, tag="bank", name="scores%d" % n)
+            nc.tensor.matmul_mx(
+                out=scores[:],
+                lhsT=x_codes[n][:].bitcast(FP8X4),
+                lhsT_scale=x_scales[n][:],
+                rhs=col_codes[:].bitcast(FP8X4),
+                rhs_scale=col_scales[:],
+                start=True,
+                stop=True,
+            )
+            scores_sb = keep.tile([P, COLUMNS], F32, name="scores_sb%d" % n)
+            copy(out=scores_sb[:], in_=scores[:])
+            nc.sync.dma_start(out=out[n], in_=scores_sb[:])
+
+        group_words(nc.vector.tensor_copy, col_grouped[:], col_planes[:])
+        finish_x(0)
+        quantise(nc, col_codes[:], col_scales[:], col_grouped[:])
+        quantise(nc, x_codes[0][:], x_scales[0][:], x_grouped[0][:])
+        score(0, nc.scalar.copy)
+        finish_x(1)
+        quantise(nc, x_codes[1][:], x_scales[1][:], x_grouped[1][:])
+        score(1, nc.vector.tensor_copy)

@@ -64,7 +64,6 @@ def tile_tromptcell_pa_s_kernel(
     with ExitStack() as ctx:
         keep = ctx.enter_context(tc.tile_pool(name="keep", bufs=1))
         banks = ctx.enter_context(tc.psum_pool(name="banks", bufs=8))
-        ctx.enter_context(tc.manual_schedule())
 
         vector_rows = keep.tile([P, P], BF16)
         vectors = keep.tile([P, VECTORS * PACK], F32)

@@ -20,7 +20,7 @@ COLUMN_TILES = COLUMNS // P
 ROW_TILES = 1 + COLUMN_TILES
 EPS = 1e-5
 RUN = 4
-SCALAR_BANKS = 3
+HALF = 256
 
 FLOPS = 2 * P * D * D + 2 * SAMPLES * P * D * D + 2 * SAMPLES * P * D * COLUMNS
 
@@ -37,6 +37,11 @@ def group_words(copy, grouped, planes):
         out=grouped.rearrange("p (c i) t -> p c t i", i=RUN),
         in_=planes.rearrange("p t (c i) -> p c t i", i=RUN),
     )
+
+
+def group_words_shared(nc, grouped, planes):
+    group_words(nc.scalar.copy, grouped[:, 0:HALF, :], planes[:, :, 0:HALF])
+    group_words(nc.vector.tensor_copy, grouped[:, HALF:, :], planes[:, :, HALF:])
 
 
 def quantise(nc, codes, scales, grouped):
@@ -183,15 +188,12 @@ def tile_tromptcell_pa_s_kernel(
 
         for r in range(2, ROW_TILES):
             statistics(r)
-        left, right = slice(0, D // 2), slice(D // 2, D)
-        group_words(nc.scalar.copy, w_prev_grouped[:, left, :], w_prev_raw[:, :, left])
         standard_deviation(1, ROW_TILES)
-        group_words(nc.scalar.copy, w_prev_grouped[:, right, :], w_prev_raw[:, :, right])
-        group_words(nc.vector.tensor_copy, w_prompt_grouped[:, left, :], w_prompt_raw[:, :, left])
-        group_words(nc.vector.tensor_copy, w_prompt_grouped[:, right, :], w_prompt_raw[:, :, right])
+        group_words_shared(nc, w_prompt_grouped[:], w_prompt_raw[:])
         nc.vector.reciprocal(out=rstd[:, 1:ROW_TILES], in_=std[:, 1:ROW_TILES])
         for r in range(1, ROW_TILES):
             normalise(r)
+        group_words_shared(nc, w_prev_grouped[:], w_prev_raw[:])
 
         prev_words = prev_raw[:].bitcast(F32)
         prev_t = banks.tile([P, SAMPLES * 2, P], F32, tag="bank")
@@ -218,7 +220,8 @@ def tile_tromptcell_pa_s_kernel(
                 scale=vector_column(LN_PROMPT_W, t),
                 bias=vector_column(LN_PROMPT_B, t),
             )
-        nc.vector.tensor_copy(
+        group_words(nc.scalar.copy, pn_grouped[:], pn_planes[:])
+        nc.scalar.copy(
             out=prev_grouped[:]
             .rearrange("p c t -> p (c t)")
             .bitcast(F32)
@@ -226,13 +229,12 @@ def tile_tromptcell_pa_s_kernel(
             in_=prev_t[:].rearrange("p (n u) w -> p n w u", u=2),
         )
         quantise(nc, w_prompt_codes[:], w_prompt_scales[:], w_prompt_grouped[:])
-        group_words(nc.vector.tensor_copy, pn_grouped[:], pn_planes[:])
-        quantise(nc, prev_codes[:], prev_scales[:], prev_grouped[:])
         quantise(nc, w_prev_codes[:], w_prev_scales[:], w_prev_grouped[:])
         quantise(nc, pn_codes[:], pn_scales[:], pn_grouped[:])
+        quantise(nc, prev_codes[:], prev_scales[:], prev_grouped[:])
 
         for t in range(PACK):
-            if t < SCALAR_BANKS:
+            if t % 2 == 0:
                 nc.scalar.activation(
                     out=col_planes[:, t, :],
                     in_=column_z_t[t][:],
@@ -282,26 +284,28 @@ def tile_tromptcell_pa_s_kernel(
                 op=ALU.add,
             )
 
-        def score(n, copy):
-            scores = banks.tile([P, COLUMNS], F32, tag="bank", name="scores%d" % n)
-            nc.tensor.matmul_mx(
-                out=scores[:],
-                lhsT=x_codes[n][:].bitcast(FP8X4),
-                lhsT_scale=x_scales[n][:],
-                rhs=col_codes[:].bitcast(FP8X4),
-                rhs_scale=col_scales[:],
-                start=True,
-                stop=True,
-            )
+        def score(n):
             scores_sb = keep.tile([P, COLUMNS], F32, name="scores_sb%d" % n)
-            copy(out=scores_sb[:], in_=scores[:])
+            for first, copy in ((0, nc.scalar.copy), (HALF, nc.vector.tensor_copy)):
+                columns = slice(first, first + HALF)
+                scores = banks.tile([P, HALF], F32, tag="bank", name="scores%d_%d" % (n, first))
+                nc.tensor.matmul_mx(
+                    out=scores[:],
+                    lhsT=x_codes[n][:].bitcast(FP8X4),
+                    lhsT_scale=x_scales[n][:],
+                    rhs=col_codes[:, columns].bitcast(FP8X4),
+                    rhs_scale=col_scales[:, columns],
+                    start=True,
+                    stop=True,
+                )
+                copy(out=scores_sb[:, columns], in_=scores[:])
             nc.sync.dma_start(out=out[n], in_=scores_sb[:])
 
-        group_words(nc.vector.tensor_copy, col_grouped[:], col_planes[:])
+        group_words_shared(nc, col_grouped[:], col_planes[:])
         finish_x(0)
         quantise(nc, col_codes[:], col_scales[:], col_grouped[:])
         quantise(nc, x_codes[0][:], x_scales[0][:], x_grouped[0][:])
-        score(0, nc.scalar.copy)
+        score(0)
         finish_x(1)
         quantise(nc, x_codes[1][:], x_scales[1][:], x_grouped[1][:])
-        score(1, nc.vector.tensor_copy)
+        score(1)

@@ -69,6 +69,7 @@ def tile_tromptcell_pa_s_kernel(
     with ExitStack() as ctx:
         keep = ctx.enter_context(tc.tile_pool(name="keep", bufs=1))
         banks = ctx.enter_context(tc.psum_pool(name="banks", bufs=8))
+        ctx.enter_context(tc.manual_schedule())
 
         vector_rows = keep.tile([P, P], BF16)
         vectors = keep.tile([P, VECTORS * PACK], F32)
@@ -136,8 +137,10 @@ def tile_tromptcell_pa_s_kernel(
 
         row_tiles = [prompt_raw[:]] + [column_raw[:, ct, :] for ct in range(COLUMN_TILES)]
 
-        def statistics(r):
+        def partial_statistics(r):
             nc.vector.bn_stats(out=stats[:, r, :], in_=row_tiles[r])
+
+        def mean_and_variance(r):
             nc.vector.bn_aggr(out=mean_var[:, r, :], in_=stats[:, r, :])
 
         def standard_deviation(first, last):
@@ -145,6 +148,9 @@ def tile_tromptcell_pa_s_kernel(
                 out=var_eps[:, first:last], in0=mean_var[:, first:last, 1], scalar1=EPS
             )
             nc.scalar.activation(out=std[:, first:last], in_=var_eps[:, first:last], func=ACT.Sqrt)
+
+        def reciprocal_std(first, last):
+            nc.vector.reciprocal(out=rstd[:, first:last], in_=std[:, first:last])
 
         def normalise(r):
             nc.vector.tensor_scalar(
@@ -159,16 +165,24 @@ def tile_tromptcell_pa_s_kernel(
         def vector_column(v, t):
             return vectors[:, PACK * v + t : PACK * v + t + 1]
 
-        statistics(0)
-        standard_deviation(0, 1)
+        partial_statistics(0)
         prompt_t = banks.tile([P, PACK, P], BF16, tag="bank")
         for t in range(PACK):
             nc.tensor.transpose(
                 out=prompt_t[:, t, :], in_=prompt_raw[:, t * P : (t + 1) * P], identity=ident_bf16[:]
             )
-        statistics(1)
-        nc.vector.reciprocal(out=rstd[:, 0:1], in_=std[:, 0:1])
+        partial_statistics(1)
+        mean_and_variance(0)
+        partial_statistics(2)
+        mean_and_variance(1)
+        standard_deviation(0, 1)
+        partial_statistics(3)
+        mean_and_variance(2)
+        reciprocal_std(0, 1)
+        partial_statistics(4)
+        mean_and_variance(3)
         normalise(0)
+        mean_and_variance(4)
 
         vectors_t = banks.tile([P, P], BF16, tag="bank")
         nc.tensor.transpose(out=vectors_t[:], in_=vector_rows[:], identity=ident_bf16[:])
@@ -186,14 +200,13 @@ def tile_tromptcell_pa_s_kernel(
                 out=prompt_z_t[:, t, :], in_=z[:, 0, t * P : (t + 1) * P], identity=ident_f32[:]
             )
 
-        for r in range(2, ROW_TILES):
-            statistics(r)
-        standard_deviation(1, ROW_TILES)
         group_words_shared(nc, w_prompt_grouped[:], w_prompt_raw[:])
-        nc.vector.reciprocal(out=rstd[:, 1:ROW_TILES], in_=std[:, 1:ROW_TILES])
+        standard_deviation(1, ROW_TILES)
+        group_words_shared(nc, w_prev_grouped[:], w_prev_raw[:])
+        reciprocal_std(1, ROW_TILES)
+        quantise(nc, w_prompt_codes[:], w_prompt_scales[:], w_prompt_grouped[:])
         for r in range(1, ROW_TILES):
             normalise(r)
-        group_words_shared(nc, w_prev_grouped[:], w_prev_raw[:])
 
         prev_words = prev_raw[:].bitcast(F32)
         prev_t = banks.tile([P, SAMPLES * 2, P], F32, tag="bank")
@@ -220,7 +233,6 @@ def tile_tromptcell_pa_s_kernel(
                 scale=vector_column(LN_PROMPT_W, t),
                 bias=vector_column(LN_PROMPT_B, t),
             )
-        group_words(nc.scalar.copy, pn_grouped[:], pn_planes[:])
         nc.scalar.copy(
             out=prev_grouped[:]
             .rearrange("p c t -> p (c t)")
@@ -228,10 +240,10 @@ def tile_tromptcell_pa_s_kernel(
             .rearrange("p (n w u) -> p n w u", n=SAMPLES, u=2),
             in_=prev_t[:].rearrange("p (n u) w -> p n w u", u=2),
         )
-        quantise(nc, w_prompt_codes[:], w_prompt_scales[:], w_prompt_grouped[:])
+        group_words(nc.scalar.copy, pn_grouped[:], pn_planes[:])
         quantise(nc, w_prev_codes[:], w_prev_scales[:], w_prev_grouped[:])
-        quantise(nc, pn_codes[:], pn_scales[:], pn_grouped[:])
         quantise(nc, prev_codes[:], prev_scales[:], prev_grouped[:])
+        quantise(nc, pn_codes[:], pn_scales[:], pn_grouped[:])
 
         for t in range(PACK):
             if t % 2 == 0:
@@ -284,13 +296,16 @@ def tile_tromptcell_pa_s_kernel(
                 op=ALU.add,
             )
 
-        def score(n):
-            scores_sb = keep.tile([P, COLUMNS], F32, name="scores_sb%d" % n)
-            for first, copy in ((0, nc.scalar.copy), (HALF, nc.vector.tensor_copy)):
+        half_starts = (0, HALF)
+        half_copies = (nc.scalar.copy, nc.vector.tensor_copy)
+
+        def multiply(n):
+            scores = []
+            for first in half_starts:
                 columns = slice(first, first + HALF)
-                scores = banks.tile([P, HALF], F32, tag="bank", name="scores%d_%d" % (n, first))
+                bank = banks.tile([P, HALF], F32, tag="bank", name="scores%d_%d" % (n, first))
                 nc.tensor.matmul_mx(
-                    out=scores[:],
+                    out=bank[:],
                     lhsT=x_codes[n][:].bitcast(FP8X4),
                     lhsT_scale=x_scales[n][:],
                     rhs=col_codes[:, columns].bitcast(FP8X4),
@@ -298,14 +313,22 @@ def tile_tromptcell_pa_s_kernel(
                     start=True,
                     stop=True,
                 )
-                copy(out=scores_sb[:, columns], in_=scores[:])
+                scores.append(bank)
+            return scores
+
+        def store(n, scores):
+            scores_sb = keep.tile([P, COLUMNS], F32, name="scores_sb%d" % n)
+            for bank, first, copy in zip(scores, half_starts, half_copies):
+                copy(out=scores_sb[:, first : first + HALF], in_=bank[:])
             nc.sync.dma_start(out=out[n], in_=scores_sb[:])
 
         group_words_shared(nc, col_grouped[:], col_planes[:])
         finish_x(0)
         quantise(nc, col_codes[:], col_scales[:], col_grouped[:])
         quantise(nc, x_codes[0][:], x_scales[0][:], x_grouped[0][:])
-        score(0)
+        scores0 = multiply(0)
         finish_x(1)
         quantise(nc, x_codes[1][:], x_scales[1][:], x_grouped[1][:])
-        score(1)
+        scores1 = multiply(1)
+        store(0, scores0)
+        store(1, scores1)

@@ -39,9 +39,9 @@ def group_words(copy, grouped, planes):
     )
 
 
-def group_words_shared(nc, grouped, planes):
-    group_words(nc.scalar.copy, grouped[:, 0:HALF, :], planes[:, :, 0:HALF])
-    group_words(nc.vector.tensor_copy, grouped[:, HALF:, :], planes[:, :, HALF:])
+def group_words_shared(nc, grouped, planes, split):
+    group_words(nc.scalar.copy, grouped[:, 0:split, :], planes[:, :, 0:split])
+    group_words(nc.vector.tensor_copy, grouped[:, split:, :], planes[:, :, split:])
 
 
 def quantise(nc, codes, scales, grouped):
@@ -68,7 +68,7 @@ def tile_tromptcell_pa_s_kernel(
     nc = tc.nc
     with ExitStack() as ctx:
         keep = ctx.enter_context(tc.tile_pool(name="keep", bufs=1))
-        banks = ctx.enter_context(tc.psum_pool(name="banks", bufs=8))
+        banks = ctx.enter_context(tc.psum_pool(name="banks", bufs=1))
         ctx.enter_context(tc.manual_schedule())
 
         vector_rows = keep.tile([P, P], BF16)
@@ -86,8 +86,11 @@ def tile_tromptcell_pa_s_kernel(
 
         stats = keep.tile([P, ROW_TILES, 6], F32)
         mean_var = keep.tile([P, ROW_TILES, 2], F32)
-        var_eps = keep.tile([P, ROW_TILES], F32)
-        std = keep.tile([P, ROW_TILES], F32)
+        eps = keep.tile([P, 1], F32)
+        row_sums = keep.tile([P, 2], F32)
+        neg_mean = keep.tile([P, 1], F32)
+        shift = keep.tile([P, 1], F32)
+        unused = keep.tile([P, D], BF16)
         rstd = keep.tile([P, ROW_TILES], F32)
         z = keep.tile([P, ROW_TILES, D], F32)
 
@@ -109,31 +112,44 @@ def tile_tromptcell_pa_s_kernel(
         x_grouped, x_codes, x_scales = zip(*[mx_operand("x%d" % n, P) for n in range(SAMPLES)])
 
         nc.gpsimd.memset(vector_rows[:], 0.0)
-        for v, vector in enumerate((ln_prompt_w, ln_prompt_b, b_imp, ln_col_w, ln_col_b)):
-            nc.scalar.dma_start(
+
+        def load_vector(v, vector):
+            nc.sync.dma_start(
                 out=vector_rows[PACK * v : PACK * (v + 1), :],
                 in_=vector.rearrange("(t p) -> t p", p=P),
             )
-        nc.sync.dma_start(out=prompt_raw[:], in_=emb_prompt)
+
         column_view = emb_column.rearrange("(ct p) f -> p ct f", p=P)
-        for first in range(0, COLUMN_TILES, 2):
+
+        def load_columns(first, last):
             nc.sync.dma_start(
-                out=column_raw[:, first : first + 2, :], in_=column_view[:, first : first + 2, :]
+                out=column_raw[:, first:last, :], in_=column_view[:, first:last, :]
             )
+
+        load_columns(0, 1)
+        nc.sync.dma_start(out=prompt_raw[:], in_=emb_prompt)
+        load_columns(1, 2)
+        load_columns(2, COLUMN_TILES)
         nc.sync.dma_start(out=w_prompt_raw[:], in_=W_imp[0:D, :].rearrange("(t p) f -> p t f", p=P))
-        nc.sync.dma_start(
-            out=w_prev_raw[:].rearrange("p (u e) f -> p u e f", u=2),
-            in_=W_imp[D : 2 * D, :].rearrange("(u p e) f -> p u e f", u=2, e=2),
-        )
+        load_vector(LN_PROMPT_W, ln_prompt_w)
+        load_vector(LN_PROMPT_B, ln_prompt_b)
+        load_vector(B_IMP, b_imp)
+        load_vector(LN_COL_W, ln_col_w)
+        load_vector(LN_COL_B, ln_col_b)
         nc.sync.dma_start(
             out=prev_raw[:].rearrange("p (n f) -> p n f", n=SAMPLES),
             in_=prev_cell_out.rearrange("n p f -> p n f"),
+        )
+        nc.sync.dma_start(
+            out=w_prev_raw[:].rearrange("p (u e) f -> p u e f", u=2),
+            in_=W_imp[D : 2 * D, :].rearrange("(u p e) f -> p u e f", u=2, e=2),
         )
 
         make_identity(nc, ident_bf16[:])
         make_identity(nc, ident_f32[:])
         nc.vector.memset(one[:], 1.0)
-        nc.scalar.activation(out=table_warmer[:], in_=one[:], func=ACT.Sqrt)
+        nc.vector.tensor_scalar(out=eps[:], in0=one[:], scalar1=EPS, scalar2=None, op0=ALU.mult)
+        nc.scalar.activation(out=table_warmer[:], in_=one[:], func=ACT.Abs_reciprocal_sqrt)
 
         row_tiles = [prompt_raw[:]] + [column_raw[:, ct, :] for ct in range(COLUMN_TILES)]
 
@@ -143,14 +159,13 @@ def tile_tromptcell_pa_s_kernel(
         def mean_and_variance(r):
             nc.vector.bn_aggr(out=mean_var[:, r, :], in_=stats[:, r, :])
 
-        def standard_deviation(first, last):
-            nc.vector.tensor_scalar_add(
-                out=var_eps[:, first:last], in0=mean_var[:, first:last, 1], scalar1=EPS
-            )
-            nc.scalar.activation(out=std[:, first:last], in_=var_eps[:, first:last], func=ACT.Sqrt)
-
         def reciprocal_std(first, last):
-            nc.vector.reciprocal(out=rstd[:, first:last], in_=std[:, first:last])
+            nc.scalar.activation(
+                out=rstd[:, first:last],
+                in_=mean_var[:, first:last, 1],
+                func=ACT.Abs_reciprocal_sqrt,
+                bias=eps[:],
+            )
 
         def normalise(r):
             nc.vector.tensor_scalar(
@@ -165,66 +180,82 @@ def tile_tromptcell_pa_s_kernel(
         def vector_column(v, t):
             return vectors[:, PACK * v + t : PACK * v + t + 1]
 
-        partial_statistics(0)
-        prompt_t = banks.tile([P, PACK, P], BF16, tag="bank")
+        nc.scalar.activation(
+            out=unused[:], in_=prompt_raw[:], func=ACT.Identity, accum_out=row_sums[:, 0:1]
+        )
+        nc.scalar.activation(
+            out=neg_mean[:], in_=row_sums[:, 0:1], func=ACT.Copy, scale=-1.0 / D
+        )
+        nc.scalar.activation(
+            out=unused[:],
+            in_=prompt_raw[:],
+            func=ACT.Square,
+            bias=neg_mean[:],
+            accum_out=row_sums[:, 1:2],
+        )
+        nc.scalar.activation(
+            out=rstd[:, 0:1],
+            in_=row_sums[:, 1:2],
+            func=ACT.Abs_reciprocal_sqrt,
+            scale=1.0 / D,
+            bias=eps[:],
+        )
+        nc.scalar.activation(out=shift[:], in_=neg_mean[:], func=ACT.Copy, scale=rstd[:, 0:1])
+        partial_statistics(1)
+        partial_statistics(2)
+        mean_and_variance(1)
+        partial_statistics(3)
+        mean_and_variance(2)
+        reciprocal_std(1, 3)
+        nc.scalar.activation(
+            out=z[:, 0, :], in_=prompt_raw[:], func=ACT.Identity, scale=rstd[:, 0:1], bias=shift[:]
+        )
+        partial_statistics(4)
+        mean_and_variance(3)
+        mean_and_variance(4)
+        normalise(1)
+        normalise(2)
+
+        prompt_t = banks.tile([P, PACK, P], BF16, tag="prompt")
         for t in range(PACK):
             nc.tensor.transpose(
                 out=prompt_t[:, t, :], in_=prompt_raw[:, t * P : (t + 1) * P], identity=ident_bf16[:]
             )
-        partial_statistics(1)
-        mean_and_variance(0)
-        partial_statistics(2)
-        mean_and_variance(1)
-        standard_deviation(0, 1)
-        partial_statistics(3)
-        mean_and_variance(2)
-        reciprocal_std(0, 1)
-        partial_statistics(4)
-        mean_and_variance(3)
-        normalise(0)
-        mean_and_variance(4)
-
-        vectors_t = banks.tile([P, P], BF16, tag="bank")
+        vectors_t = banks.tile([P, P], BF16, tag="vectors")
         nc.tensor.transpose(out=vectors_t[:], in_=vector_rows[:], identity=ident_bf16[:])
         nc.scalar.copy(out=vectors[:], in_=vectors_t[:, 0 : VECTORS * PACK])
-        for t in range(PACK):
-            nc.scalar.activation(
-                out=residual[:, t, :],
-                in_=prompt_t[:, t, :],
-                func=ACT.Identity,
-                bias=vector_column(B_IMP, t),
-            )
-        prompt_z_t = banks.tile([P, PACK, P], F32, tag="bank")
+        reciprocal_std(3, ROW_TILES)
+        normalise(3)
+        normalise(4)
+
+        prompt_z_t = banks.tile([P, PACK, P], F32, tag="prompt_z")
         for t in range(PACK):
             nc.tensor.transpose(
                 out=prompt_z_t[:, t, :], in_=z[:, 0, t * P : (t + 1) * P], identity=ident_f32[:]
             )
+        column_z_t = [
+            banks.tile([P, COLUMNS], F32, tag="column%d" % t, name="column_z_t%d" % t) for t in range(PACK)
+        ]
 
-        group_words_shared(nc, w_prompt_grouped[:], w_prompt_raw[:])
-        standard_deviation(1, ROW_TILES)
-        group_words_shared(nc, w_prev_grouped[:], w_prev_raw[:])
-        reciprocal_std(1, ROW_TILES)
-        quantise(nc, w_prompt_codes[:], w_prompt_scales[:], w_prompt_grouped[:])
-        for r in range(1, ROW_TILES):
-            normalise(r)
+        def transpose_columns(r):
+            for t in range(PACK):
+                nc.tensor.transpose(
+                    out=column_z_t[t][:, (r - 1) * P : r * P],
+                    in_=z[:, r, t * P : (t + 1) * P],
+                    identity=ident_f32[:],
+                )
 
+        for r in range(1, ROW_TILES - 1):
+            transpose_columns(r)
         prev_words = prev_raw[:].bitcast(F32)
-        prev_t = banks.tile([P, SAMPLES * 2, P], F32, tag="bank")
+        prev_t = banks.tile([P, SAMPLES * 2, P], F32, tag="prev")
         for j in range(SAMPLES * 2):
             nc.tensor.transpose(
                 out=prev_t[:, j, :], in_=prev_words[:, j * P : (j + 1) * P], identity=ident_f32[:]
             )
-        column_z_t = [
-            banks.tile([P, COLUMNS], F32, tag="bank", name="column_z_t%d" % t) for t in range(PACK)
-        ]
-        for ct in range(COLUMN_TILES):
-            for t in range(PACK):
-                nc.tensor.transpose(
-                    out=column_z_t[t][:, ct * P : (ct + 1) * P],
-                    in_=z[:, 1 + ct, t * P : (t + 1) * P],
-                    identity=ident_f32[:],
-                )
+        transpose_columns(ROW_TILES - 1)
 
+        group_words_shared(nc, w_prompt_grouped[:], w_prompt_raw[:], HALF)
         for t in range(PACK):
             nc.scalar.activation(
                 out=pn_planes[:, t, :],
@@ -240,10 +271,20 @@ def tile_tromptcell_pa_s_kernel(
             .rearrange("p (n w u) -> p n w u", n=SAMPLES, u=2),
             in_=prev_t[:].rearrange("p (n u) w -> p n w u", u=2),
         )
-        group_words(nc.scalar.copy, pn_grouped[:], pn_planes[:])
+        group_words_shared(nc, w_prev_grouped[:], w_prev_raw[:], HALF)
+        quantise(nc, w_prompt_codes[:], w_prompt_scales[:], w_prompt_grouped[:])
+        group_words(nc.vector.tensor_copy, pn_grouped[:], pn_planes[:])
         quantise(nc, w_prev_codes[:], w_prev_scales[:], w_prev_grouped[:])
-        quantise(nc, prev_codes[:], prev_scales[:], prev_grouped[:])
         quantise(nc, pn_codes[:], pn_scales[:], pn_grouped[:])
+        quantise(nc, prev_codes[:], prev_scales[:], prev_grouped[:])
+
+        for t in range(PACK):
+            nc.scalar.activation(
+                out=residual[:, t, :],
+                in_=prompt_t[:, t, :],
+                func=ACT.Identity,
+                bias=vector_column(B_IMP, t),
+            )
 
         for t in range(PACK):
             if t % 2 == 0:
@@ -264,7 +305,10 @@ def tile_tromptcell_pa_s_kernel(
                     op1=ALU.add,
                 )
 
-        x_t = [banks.tile([P, PACK, P], F32, tag="bank", name="x_t%d" % n) for n in range(SAMPLES)]
+        x_t = [
+            banks.tile([P, PACK, P], F32, tag=tag, name="x_t%d" % n)
+            for n, tag in enumerate(("vectors", "prompt_z"))
+        ]
         for n in range(SAMPLES):
             prompts = slice(n * P, (n + 1) * P)
             for t in range(PACK):
@@ -297,13 +341,14 @@ def tile_tromptcell_pa_s_kernel(
             )
 
         half_starts = (0, HALF)
-        half_copies = (nc.scalar.copy, nc.vector.tensor_copy)
 
         def multiply(n):
             scores = []
-            for first in half_starts:
+            for half, first in enumerate(half_starts):
                 columns = slice(first, first + HALF)
-                bank = banks.tile([P, HALF], F32, tag="bank", name="scores%d_%d" % (n, first))
+                bank = banks.tile(
+                    [P, HALF], F32, tag="column%d" % (2 * n + half), name="scores%d_%d" % (n, half)
+                )
                 nc.tensor.matmul_mx(
                     out=bank[:],
                     lhsT=x_codes[n][:].bitcast(FP8X4),
@@ -316,19 +361,19 @@ def tile_tromptcell_pa_s_kernel(
                 scores.append(bank)
             return scores
 
-        def store(n, scores):
+        def store(n, scores, half_copies):
             scores_sb = keep.tile([P, COLUMNS], F32, name="scores_sb%d" % n)
             for bank, first, copy in zip(scores, half_starts, half_copies):
                 copy(out=scores_sb[:, first : first + HALF], in_=bank[:])
             nc.sync.dma_start(out=out[n], in_=scores_sb[:])
 
-        group_words_shared(nc, col_grouped[:], col_planes[:])
         finish_x(0)
+        group_words_shared(nc, col_grouped[:], col_planes[:], HALF)
+        finish_x(1)
         quantise(nc, col_codes[:], col_scales[:], col_grouped[:])
         quantise(nc, x_codes[0][:], x_scales[0][:], x_grouped[0][:])
-        scores0 = multiply(0)
-        finish_x(1)
         quantise(nc, x_codes[1][:], x_scales[1][:], x_grouped[1][:])
+        scores0 = multiply(0)
         scores1 = multiply(1)
-        store(0, scores0)
-        store(1, scores1)
+        store(0, scores0, (nc.scalar.copy, nc.vector.tensor_copy))
+        store(1, scores1, (nc.scalar.copy, nc.vector.tensor_copy))

@@ -20,6 +20,8 @@ COLUMN_TILES = COLUMNS // P
 ROW_TILES = 1 + COLUMN_TILES
 EPS = 1e-5
 RUN = 4
+W_PROMPT_SPLIT = 320
+COL_SPLIT = 320
 HALF = 256
 
 FLOPS = 2 * P * D * D + 2 * SAMPLES * P * D * D + 2 * SAMPLES * P * D * COLUMNS
@@ -88,8 +90,6 @@ def tile_tromptcell_pa_s_kernel(
         mean_var = keep.tile([P, ROW_TILES, 2], F32)
         eps = keep.tile([P, 1], F32)
         row_sums = keep.tile([P, 2], F32)
-        neg_mean = keep.tile([P, 1], F32)
-        shift = keep.tile([P, 1], F32)
         unused = keep.tile([P, D], BF16)
         rstd = keep.tile([P, ROW_TILES], F32)
         z = keep.tile([P, ROW_TILES, D], F32)
@@ -109,7 +109,7 @@ def tile_tromptcell_pa_s_kernel(
         w_prompt_grouped, w_prompt_codes, w_prompt_scales = mx_operand("w_prompt", D)
         w_prev_grouped, w_prev_codes, w_prev_scales = mx_operand("w_prev", D)
         col_grouped, col_codes, col_scales = mx_operand("col", COLUMNS)
-        x_grouped, x_codes, x_scales = zip(*[mx_operand("x%d" % n, P) for n in range(SAMPLES)])
+        x_grouped, x_codes, x_scales = mx_operand("x", SAMPLES * P)
 
         nc.gpsimd.memset(vector_rows[:], 0.0)
 
@@ -129,10 +129,10 @@ def tile_tromptcell_pa_s_kernel(
         load_columns(0, 1)
         nc.sync.dma_start(out=prompt_raw[:], in_=emb_prompt)
         load_columns(1, 2)
-        load_columns(2, COLUMN_TILES)
-        nc.sync.dma_start(out=w_prompt_raw[:], in_=W_imp[0:D, :].rearrange("(t p) f -> p t f", p=P))
         load_vector(LN_PROMPT_W, ln_prompt_w)
         load_vector(LN_PROMPT_B, ln_prompt_b)
+        nc.sync.dma_start(out=w_prompt_raw[:], in_=W_imp[0:D, :].rearrange("(t p) f -> p t f", p=P))
+        load_columns(2, COLUMN_TILES)
         load_vector(B_IMP, b_imp)
         load_vector(LN_COL_W, ln_col_w)
         load_vector(LN_COL_B, ln_col_b)
@@ -184,15 +184,21 @@ def tile_tromptcell_pa_s_kernel(
             out=unused[:], in_=prompt_raw[:], func=ACT.Identity, accum_out=row_sums[:, 0:1]
         )
         nc.scalar.activation(
-            out=neg_mean[:], in_=row_sums[:, 0:1], func=ACT.Copy, scale=-1.0 / D
+            out=mean_var[:, 0, 0:1], in_=row_sums[:, 0:1], func=ACT.Copy, scale=1.0 / D
         )
         nc.scalar.activation(
             out=unused[:],
             in_=prompt_raw[:],
             func=ACT.Square,
-            bias=neg_mean[:],
+            scale=-1.0,
+            bias=mean_var[:, 0, 0:1],
             accum_out=row_sums[:, 1:2],
         )
+        partial_statistics(1)
+        partial_statistics(2)
+        mean_and_variance(1)
+        mean_and_variance(2)
+        reciprocal_std(1, 3)
         nc.scalar.activation(
             out=rstd[:, 0:1],
             in_=row_sums[:, 1:2],
@@ -200,21 +206,6 @@ def tile_tromptcell_pa_s_kernel(
             scale=1.0 / D,
             bias=eps[:],
         )
-        nc.scalar.activation(out=shift[:], in_=neg_mean[:], func=ACT.Copy, scale=rstd[:, 0:1])
-        partial_statistics(1)
-        partial_statistics(2)
-        mean_and_variance(1)
-        partial_statistics(3)
-        mean_and_variance(2)
-        reciprocal_std(1, 3)
-        nc.scalar.activation(
-            out=z[:, 0, :], in_=prompt_raw[:], func=ACT.Identity, scale=rstd[:, 0:1], bias=shift[:]
-        )
-        partial_statistics(4)
-        mean_and_variance(3)
-        mean_and_variance(4)
-        normalise(1)
-        normalise(2)
 
         prompt_t = banks.tile([P, PACK, P], BF16, tag="prompt")
         for t in range(PACK):
@@ -223,10 +214,15 @@ def tile_tromptcell_pa_s_kernel(
             )
         vectors_t = banks.tile([P, P], BF16, tag="vectors")
         nc.tensor.transpose(out=vectors_t[:], in_=vector_rows[:], identity=ident_bf16[:])
-        nc.scalar.copy(out=vectors[:], in_=vectors_t[:, 0 : VECTORS * PACK])
-        reciprocal_std(3, ROW_TILES)
-        normalise(3)
-        normalise(4)
+
+        group_words_shared(nc, w_prompt_grouped[:], w_prompt_raw[:], W_PROMPT_SPLIT)
+        normalise(0)
+        normalise(1)
+        partial_statistics(3)
+        normalise(2)
+        partial_statistics(4)
+        mean_and_variance(3)
+        mean_and_variance(4)
 
         prompt_z_t = banks.tile([P, PACK, P], F32, tag="prompt_z")
         for t in range(PACK):
@@ -234,7 +230,8 @@ def tile_tromptcell_pa_s_kernel(
                 out=prompt_z_t[:, t, :], in_=z[:, 0, t * P : (t + 1) * P], identity=ident_f32[:]
             )
         column_z_t = [
-            banks.tile([P, COLUMNS], F32, tag="column%d" % t, name="column_z_t%d" % t) for t in range(PACK)
+            banks.tile([P, COLUMNS], F32, tag="column%d" % t, name="column_z_t%d" % t)
+            for t in range(PACK)
         ]
 
         def transpose_columns(r):
@@ -245,17 +242,24 @@ def tile_tromptcell_pa_s_kernel(
                     identity=ident_f32[:],
                 )
 
-        for r in range(1, ROW_TILES - 1):
-            transpose_columns(r)
+        transpose_columns(1)
+        transpose_columns(2)
         prev_words = prev_raw[:].bitcast(F32)
         prev_t = banks.tile([P, SAMPLES * 2, P], F32, tag="prev")
         for j in range(SAMPLES * 2):
             nc.tensor.transpose(
                 out=prev_t[:, j, :], in_=prev_words[:, j * P : (j + 1) * P], identity=ident_f32[:]
             )
-        transpose_columns(ROW_TILES - 1)
 
-        group_words_shared(nc, w_prompt_grouped[:], w_prompt_raw[:], HALF)
+        nc.scalar.copy(out=vectors[:], in_=vectors_t[:, 0 : VECTORS * PACK])
+        for t in range(PACK):
+            nc.scalar.activation(
+                out=residual[:, t, :],
+                in_=prompt_t[:, t, :],
+                func=ACT.Identity,
+                bias=vector_column(B_IMP, t),
+            )
+        reciprocal_std(3, ROW_TILES)
         for t in range(PACK):
             nc.scalar.activation(
                 out=pn_planes[:, t, :],
@@ -271,23 +275,19 @@ def tile_tromptcell_pa_s_kernel(
             .rearrange("p (n w u) -> p n w u", n=SAMPLES, u=2),
             in_=prev_t[:].rearrange("p (n u) w -> p n w u", u=2),
         )
-        group_words_shared(nc, w_prev_grouped[:], w_prev_raw[:], HALF)
         quantise(nc, w_prompt_codes[:], w_prompt_scales[:], w_prompt_grouped[:])
+        normalise(3)
+        normalise(4)
+        transpose_columns(3)
+        transpose_columns(4)
         group_words(nc.vector.tensor_copy, pn_grouped[:], pn_planes[:])
-        quantise(nc, w_prev_codes[:], w_prev_scales[:], w_prev_grouped[:])
+        group_words_shared(nc, w_prev_grouped[:], w_prev_raw[:], HALF)
         quantise(nc, pn_codes[:], pn_scales[:], pn_grouped[:])
         quantise(nc, prev_codes[:], prev_scales[:], prev_grouped[:])
+        quantise(nc, w_prev_codes[:], w_prev_scales[:], w_prev_grouped[:])
 
         for t in range(PACK):
-            nc.scalar.activation(
-                out=residual[:, t, :],
-                in_=prompt_t[:, t, :],
-                func=ACT.Identity,
-                bias=vector_column(B_IMP, t),
-            )
-
-        for t in range(PACK):
-            if t % 2 == 0:
+            if t < PACK - 1:
                 nc.scalar.activation(
                     out=col_planes[:, t, :],
                     in_=column_z_t[t][:],
@@ -334,46 +334,40 @@ def tile_tromptcell_pa_s_kernel(
 
         def finish_x(n):
             nc.vector.tensor_tensor(
-                out=x_grouped[n][:],
+                out=x_grouped[:, n * P : (n + 1) * P, :],
                 in0=x_t[n][:].rearrange("p t w -> p w t"),
                 in1=residual[:].rearrange("p t w -> p w t"),
                 op=ALU.add,
             )
 
-        half_starts = (0, HALF)
-
-        def multiply(n):
+        group_words_shared(nc, col_grouped[:], col_planes[:], COL_SPLIT)
+        for n in range(SAMPLES):
+            finish_x(n)
+        quantise(nc, x_codes[:], x_scales[:], x_grouped[:])
+        scores_sb = [
+            keep.tile([P, COLUMNS], F32, name="scores_sb%d" % n) for n in range(SAMPLES)
+        ]
+        copies = ((nc.scalar.copy, nc.scalar.copy), (nc.vector.tensor_copy, nc.scalar.copy))
+        for half in range(2):
+            columns = slice(half * HALF, (half + 1) * HALF)
+            quantise(nc, col_codes[:, columns], col_scales[:, columns], col_grouped[:, columns, :])
             scores = []
-            for half, first in enumerate(half_starts):
-                columns = slice(first, first + HALF)
+            for n in range(SAMPLES):
+                prompts = slice(n * P, (n + 1) * P)
                 bank = banks.tile(
-                    [P, HALF], F32, tag="column%d" % (2 * n + half), name="scores%d_%d" % (n, half)
+                    [P, HALF], F32, tag="column%d" % (2 * half + n), name="scores%d_%d" % (n, half)
                 )
                 nc.tensor.matmul_mx(
                     out=bank[:],
-                    lhsT=x_codes[n][:].bitcast(FP8X4),
-                    lhsT_scale=x_scales[n][:],
+                    lhsT=x_codes[:, prompts].bitcast(FP8X4),
+                    lhsT_scale=x_scales[:, prompts],
                     rhs=col_codes[:, columns].bitcast(FP8X4),
                     rhs_scale=col_scales[:, columns],
                     start=True,
                     stop=True,
                 )
                 scores.append(bank)
-            return scores
-
-        def store(n, scores, half_copies):
-            scores_sb = keep.tile([P, COLUMNS], F32, name="scores_sb%d" % n)
-            for bank, first, copy in zip(scores, half_starts, half_copies):
-                copy(out=scores_sb[:, first : first + HALF], in_=bank[:])
-            nc.sync.dma_start(out=out[n], in_=scores_sb[:])
-
-        finish_x(0)
-        group_words_shared(nc, col_grouped[:], col_planes[:], HALF)
-        finish_x(1)
-        quantise(nc, col_codes[:], col_scales[:], col_grouped[:])
-        quantise(nc, x_codes[0][:], x_scales[0][:], x_grouped[0][:])
-        quantise(nc, x_codes[1][:], x_scales[1][:], x_grouped[1][:])
-        scores0 = multiply(0)
-        scores1 = multiply(1)
-        store(0, scores0, (nc.scalar.copy, nc.vector.tensor_copy))
-        store(1, scores1, (nc.scalar.copy, nc.vector.tensor_copy))
+            for n in range(SAMPLES):
+                copies[half][n](out=scores_sb[n][:, columns], in_=scores[n][:])
+        for n in range(SAMPLES):
+            nc.sync.dma_start(out=out[n], in_=scores_sb[n][:])

@@ -21,6 +21,7 @@ ROW_TILES = 1 + COLUMN_TILES
 EPS = 1e-5
 RUN = 4
 W_PROMPT_SPLIT = 320
+W_PREV_SPLIT = 192
 COL_SPLIT = 320
 HALF = 256
 
@@ -229,6 +230,12 @@ def tile_tromptcell_pa_s_kernel(
             nc.tensor.transpose(
                 out=prompt_z_t[:, t, :], in_=z[:, 0, t * P : (t + 1) * P], identity=ident_f32[:]
             )
+        prev_words = prev_raw[:].bitcast(F32)
+        prev_t = banks.tile([P, SAMPLES * 2, P], F32, tag="prev")
+        for j in range(SAMPLES * 2):
+            nc.tensor.transpose(
+                out=prev_t[:, j, :], in_=prev_words[:, j * P : (j + 1) * P], identity=ident_f32[:]
+            )
         column_z_t = [
             banks.tile([P, COLUMNS], F32, tag="column%d" % t, name="column_z_t%d" % t)
             for t in range(PACK)
@@ -244,22 +251,7 @@ def tile_tromptcell_pa_s_kernel(
 
         transpose_columns(1)
         transpose_columns(2)
-        prev_words = prev_raw[:].bitcast(F32)
-        prev_t = banks.tile([P, SAMPLES * 2, P], F32, tag="prev")
-        for j in range(SAMPLES * 2):
-            nc.tensor.transpose(
-                out=prev_t[:, j, :], in_=prev_words[:, j * P : (j + 1) * P], identity=ident_f32[:]
-            )
-
         nc.scalar.copy(out=vectors[:], in_=vectors_t[:, 0 : VECTORS * PACK])
-        for t in range(PACK):
-            nc.scalar.activation(
-                out=residual[:, t, :],
-                in_=prompt_t[:, t, :],
-                func=ACT.Identity,
-                bias=vector_column(B_IMP, t),
-            )
-        reciprocal_std(3, ROW_TILES)
         for t in range(PACK):
             nc.scalar.activation(
                 out=pn_planes[:, t, :],
@@ -275,16 +267,24 @@ def tile_tromptcell_pa_s_kernel(
             .rearrange("p (n w u) -> p n w u", n=SAMPLES, u=2),
             in_=prev_t[:].rearrange("p (n u) w -> p n w u", u=2),
         )
-        quantise(nc, w_prompt_codes[:], w_prompt_scales[:], w_prompt_grouped[:])
+        reciprocal_std(3, ROW_TILES)
+        group_words(nc.scalar.copy, pn_grouped[:], pn_planes[:])
+        group_words_shared(nc, w_prev_grouped[:], w_prev_raw[:], W_PREV_SPLIT)
         normalise(3)
         normalise(4)
         transpose_columns(3)
         transpose_columns(4)
-        group_words(nc.vector.tensor_copy, pn_grouped[:], pn_planes[:])
-        group_words_shared(nc, w_prev_grouped[:], w_prev_raw[:], HALF)
-        quantise(nc, pn_codes[:], pn_scales[:], pn_grouped[:])
+        quantise(nc, w_prompt_codes[:], w_prompt_scales[:], w_prompt_grouped[:])
         quantise(nc, prev_codes[:], prev_scales[:], prev_grouped[:])
+        quantise(nc, pn_codes[:], pn_scales[:], pn_grouped[:])
         quantise(nc, w_prev_codes[:], w_prev_scales[:], w_prev_grouped[:])
+        for t in range(PACK):
+            nc.scalar.activation(
+                out=residual[:, t, :],
+                in_=prompt_t[:, t, :],
+                func=ACT.Identity,
+                bias=vector_column(B_IMP, t),
+            )
 
         for t in range(PACK):
             if t < PACK - 1:
@@ -340,25 +340,22 @@ def tile_tromptcell_pa_s_kernel(
                 op=ALU.add,
             )
 
-        group_words_shared(nc, col_grouped[:], col_planes[:], COL_SPLIT)
+        group_words(nc.scalar.copy, col_grouped[:, 0:COL_SPLIT, :], col_planes[:, :, 0:COL_SPLIT])
         for n in range(SAMPLES):
             finish_x(n)
+        group_words(nc.vector.tensor_copy, col_grouped[:, COL_SPLIT:, :], col_planes[:, :, COL_SPLIT:])
         quantise(nc, x_codes[:], x_scales[:], x_grouped[:])
-        scores_sb = [
-            keep.tile([P, COLUMNS], F32, name="scores_sb%d" % n) for n in range(SAMPLES)
-        ]
-        copies = ((nc.scalar.copy, nc.scalar.copy), (nc.vector.tensor_copy, nc.scalar.copy))
+        pending = []
         for half in range(2):
             columns = slice(half * HALF, (half + 1) * HALF)
             quantise(nc, col_codes[:, columns], col_scales[:, columns], col_grouped[:, columns, :])
-            scores = []
-            for n in range(SAMPLES):
+            for n, copy in enumerate((nc.scalar.copy, nc.vector.tensor_copy)):
                 prompts = slice(n * P, (n + 1) * P)
-                bank = banks.tile(
+                scores = banks.tile(
                     [P, HALF], F32, tag="column%d" % (2 * half + n), name="scores%d_%d" % (n, half)
                 )
                 nc.tensor.matmul_mx(
-                    out=bank[:],
+                    out=scores[:],
                     lhsT=x_codes[:, prompts].bitcast(FP8X4),
                     lhsT_scale=x_scales[:, prompts],
                     rhs=col_codes[:, columns].bitcast(FP8X4),
@@ -366,8 +363,8 @@ def tile_tromptcell_pa_s_kernel(
                     start=True,
                     stop=True,
                 )
-                scores.append(bank)
-            for n in range(SAMPLES):
-                copies[half][n](out=scores_sb[n][:, columns], in_=scores[n][:])
-        for n in range(SAMPLES):
-            nc.sync.dma_start(out=out[n], in_=scores_sb[n][:])
+                scores_sb = keep.tile([P, HALF], F32, name="scores_sb%d_%d" % (n, half))
+                pending.append((copy, scores_sb, scores, out[n, :, columns]))
+        for copy, scores_sb, scores, destination in pending:
+            copy(out=scores_sb[:], in_=scores[:])
+            nc.sync.dma_start(out=destination, in_=scores_sb[:])

@@ -208,6 +208,14 @@ def tile_tromptcell_pa_s_kernel(
             bias=eps[:],
         )
 
+        def warm(tag, passes):
+            unread = banks.tile([P, P], F32, tag=tag, name="unread_" + tag)
+            for i in range(passes):
+                nc.tensor.matmul(
+                    out=unread[:], lhsT=ident_f32[:], rhs=ident_f32[:], start=True, stop=True
+                )
+
+        warm("prev", 2)
         prompt_t = banks.tile([P, PACK, P], BF16, tag="prompt")
         for t in range(PACK):
             nc.tensor.transpose(
@@ -251,6 +259,7 @@ def tile_tromptcell_pa_s_kernel(
 
         transpose_columns(1)
         transpose_columns(2)
+        warm("vectors", 3)
         nc.scalar.copy(out=vectors[:], in_=vectors_t[:, 0 : VECTORS * PACK])
         for t in range(PACK):
             nc.scalar.activation(
@@ -331,6 +340,8 @@ def tile_tromptcell_pa_s_kernel(
                     start=False,
                     stop=True,
                 )
+
+        warm("prompt", 2)
 
         def finish_x(n):
             nc.vector.tensor_tensor(

@@ -209,7 +209,7 @@ def tile_tromptcell_pa_s_kernel(
         )
 
         def warm(tag, passes):
-            unread = banks.tile([P, P], F32, tag=tag, name="unread_" + tag)
+            unread = banks.tile([P, P], F32, tag=tag, name="unread%d" % passes)
             for i in range(passes):
                 nc.tensor.matmul(
                     out=unread[:], lhsT=ident_f32[:], rhs=ident_f32[:], start=True, stop=True
@@ -221,6 +221,7 @@ def tile_tromptcell_pa_s_kernel(
             nc.tensor.transpose(
                 out=prompt_t[:, t, :], in_=prompt_raw[:, t * P : (t + 1) * P], identity=ident_bf16[:]
             )
+        warm("prev", 2)
         vectors_t = banks.tile([P, P], BF16, tag="vectors")
         nc.tensor.transpose(out=vectors_t[:], in_=vector_rows[:], identity=ident_bf16[:])
 
@@ -341,7 +342,17 @@ def tile_tromptcell_pa_s_kernel(
                     stop=True,
                 )
 
-        warm("prompt", 2)
+        unread = banks.tile([P, D], F32, tag="prompt", name="unread_mx")
+        for i in range(3):
+            nc.tensor.matmul_mx(
+                out=unread[:],
+                lhsT=w_prompt_codes[:, 0:P].bitcast(FP8X4),
+                lhsT_scale=w_prompt_scales[:, 0:P],
+                rhs=w_prompt_codes[:].bitcast(FP8X4),
+                rhs_scale=w_prompt_scales[:],
+                start=True,
+                stop=True,
+            )
 
         def finish_x(n):
             nc.vector.tensor_tensor(

@@ -229,8 +229,8 @@ def tile_tromptcell_pa_s_kernel(
         normalise(0)
         normalise(1)
         partial_statistics(3)
-        normalise(2)
         partial_statistics(4)
+        normalise(2)
         mean_and_variance(3)
         mean_and_variance(4)
 
@@ -260,7 +260,7 @@ def tile_tromptcell_pa_s_kernel(
 
         transpose_columns(1)
         transpose_columns(2)
-        warm("vectors", 3)
+        warm("vectors", 4)
         nc.scalar.copy(out=vectors[:], in_=vectors_t[:, 0 : VECTORS * PACK])
         for t in range(PACK):
             nc.scalar.activation(
@@ -315,6 +315,20 @@ def tile_tromptcell_pa_s_kernel(
                     op1=ALU.add,
                 )
 
+        def warm_mx(tag, passes):
+            unread = banks.tile([P, D], F32, tag=tag, name="unread_mx_" + tag)
+            for i in range(passes):
+                nc.tensor.matmul_mx(
+                    out=unread[:],
+                    lhsT=w_prompt_codes[:, 0:P].bitcast(FP8X4),
+                    lhsT_scale=w_prompt_scales[:, 0:P],
+                    rhs=w_prompt_codes[:].bitcast(FP8X4),
+                    rhs_scale=w_prompt_scales[:],
+                    start=True,
+                    stop=True,
+                )
+
+        warm_mx("prev", 1)
         x_t = [
             banks.tile([P, PACK, P], F32, tag=tag, name="x_t%d" % n)
             for n, tag in enumerate(("vectors", "prompt_z"))
@@ -342,17 +356,7 @@ def tile_tromptcell_pa_s_kernel(
                     stop=True,
                 )
 
-        unread = banks.tile([P, D], F32, tag="prompt", name="unread_mx")
-        for i in range(3):
-            nc.tensor.matmul_mx(
-                out=unread[:],
-                lhsT=w_prompt_codes[:, 0:P].bitcast(FP8X4),
-                lhsT_scale=w_prompt_scales[:, 0:P],
-                rhs=w_prompt_codes[:].bitcast(FP8X4),
-                rhs_scale=w_prompt_scales[:],
-                start=True,
-                stop=True,
-            )
+        warm_mx("prompt", 3)
 
         def finish_x(n):
             nc.vector.tensor_tensor(

@@ -22,7 +22,7 @@ EPS = 1e-5
 RUN = 4
 W_PROMPT_SPLIT = 320
 W_PREV_SPLIT = 192
-COL_SPLIT = 320
+COL_SPLIT = 384
 HALF = 256
 
 FLOPS = 2 * P * D * D + 2 * SAMPLES * P * D * D + 2 * SAMPLES * P * D * COLUMNS
@@ -360,13 +360,16 @@ def tile_tromptcell_pa_s_kernel(
 
         def finish_x(n):
             nc.vector.tensor_tensor(
-                out=x_grouped[:, n * P : (n + 1) * P, :],
-                in0=x_t[n][:].rearrange("p t w -> p w t"),
-                in1=residual[:].rearrange("p t w -> p w t"),
+                out=x_grouped[:, n * P : (n + 1) * P, :].rearrange("p (c i) t -> p c t i", i=RUN),
+                in0=x_t[n][:].rearrange("p t (c i) -> p c t i", i=RUN),
+                in1=residual[:].rearrange("p t (c i) -> p c t i", i=RUN),
                 op=ALU.add,
             )
 
-        group_words(nc.scalar.copy, col_grouped[:, 0:COL_SPLIT, :], col_planes[:, :, 0:COL_SPLIT])
+        for first, last in ((0, HALF), (HALF, COL_SPLIT)):
+            group_words(
+                nc.scalar.copy, col_grouped[:, first:last, :], col_planes[:, :, first:last]
+            )
         for n in range(SAMPLES):
             finish_x(n)
         group_words(nc.vector.tensor_copy, col_grouped[:, COL_SPLIT:, :], col_planes[:, :, COL_SPLIT:])

@@ -20,9 +20,10 @@ COLUMN_TILES = COLUMNS // P
 ROW_TILES = 1 + COLUMN_TILES
 EPS = 1e-5
 RUN = 4
-W_PROMPT_SPLIT = 320
-W_PREV_SPLIT = 192
-COL_SPLIT = 384
+W_PROMPT_SPLIT = 192
+W_PREV_SPLIT = 0
+COL0_SPLIT = 0
+COL1_SPLIT = 192
 HALF = 256
 
 FLOPS = 2 * P * D * D + 2 * SAMPLES * P * D * D + 2 * SAMPLES * P * D * COLUMNS
@@ -43,8 +44,10 @@ def group_words(copy, grouped, planes):
 
 
 def group_words_shared(nc, grouped, planes, split):
-    group_words(nc.scalar.copy, grouped[:, 0:split, :], planes[:, :, 0:split])
-    group_words(nc.vector.tensor_copy, grouped[:, split:, :], planes[:, :, split:])
+    if split > 0:
+        group_words(nc.scalar.copy, grouped[:, 0:split, :], planes[:, :, 0:split])
+    if split < grouped.shape[1]:
+        group_words(nc.vector.tensor_copy, grouped[:, split:, :], planes[:, :, split:])
 
 
 def quantise(nc, codes, scales, grouped):
@@ -130,17 +133,15 @@ def tile_tromptcell_pa_s_kernel(
         load_columns(0, 1)
         nc.sync.dma_start(out=prompt_raw[:], in_=emb_prompt)
         load_columns(1, 2)
+        load_columns(2, COLUMN_TILES)
         load_vector(LN_PROMPT_W, ln_prompt_w)
         load_vector(LN_PROMPT_B, ln_prompt_b)
-        nc.sync.dma_start(out=w_prompt_raw[:], in_=W_imp[0:D, :].rearrange("(t p) f -> p t f", p=P))
-        load_columns(2, COLUMN_TILES)
         load_vector(B_IMP, b_imp)
-        load_vector(LN_COL_W, ln_col_w)
-        load_vector(LN_COL_B, ln_col_b)
         nc.sync.dma_start(
             out=prev_raw[:].rearrange("p (n f) -> p n f", n=SAMPLES),
             in_=prev_cell_out.rearrange("n p f -> p n f"),
         )
+        nc.sync.dma_start(out=w_prompt_raw[:], in_=W_imp[0:D, :].rearrange("(t p) f -> p t f", p=P))
         nc.sync.dma_start(
             out=w_prev_raw[:].rearrange("p (u e) f -> p u e f", u=2),
             in_=W_imp[D : 2 * D, :].rearrange("(u p e) f -> p u e f", u=2, e=2),
@@ -182,30 +183,22 @@ def tile_tromptcell_pa_s_kernel(
             return vectors[:, PACK * v + t : PACK * v + t + 1]
 
         nc.scalar.activation(
-            out=unused[:], in_=prompt_raw[:], func=ACT.Identity, accum_out=row_sums[:, 0:1]
-        )
-        nc.scalar.activation(
-            out=mean_var[:, 0, 0:1], in_=row_sums[:, 0:1], func=ACT.Copy, scale=1.0 / D
+            out=unused[:],
+            in_=prompt_raw[:],
+            func=ACT.Identity,
+            scale=-1.0,
+            accum_out=row_sums[:, 0:1],
         )
         nc.scalar.activation(
             out=unused[:],
             in_=prompt_raw[:],
             func=ACT.Square,
-            scale=-1.0,
-            bias=mean_var[:, 0, 0:1],
+            scale=float(D),
+            bias=row_sums[:, 0:1],
             accum_out=row_sums[:, 1:2],
         )
-        partial_statistics(1)
-        partial_statistics(2)
-        mean_and_variance(1)
-        mean_and_variance(2)
-        reciprocal_std(1, 3)
         nc.scalar.activation(
-            out=rstd[:, 0:1],
-            in_=row_sums[:, 1:2],
-            func=ACT.Abs_reciprocal_sqrt,
-            scale=1.0 / D,
-            bias=eps[:],
+            out=mean_var[:, 0, 0:1], in_=row_sums[:, 0:1], func=ACT.Copy, scale=-1.0 / D
         )
 
         def warm(tag, passes):
@@ -215,53 +208,99 @@ def tile_tromptcell_pa_s_kernel(
                     out=unread[:], lhsT=ident_f32[:], rhs=ident_f32[:], start=True, stop=True
                 )
 
-        warm("prev", 2)
         prompt_t = banks.tile([P, PACK, P], BF16, tag="prompt")
-        for t in range(PACK):
-            nc.tensor.transpose(
-                out=prompt_t[:, t, :], in_=prompt_raw[:, t * P : (t + 1) * P], identity=ident_bf16[:]
-            )
-        warm("prev", 2)
-        vectors_t = banks.tile([P, P], BF16, tag="vectors")
-        nc.tensor.transpose(out=vectors_t[:], in_=vector_rows[:], identity=ident_bf16[:])
-
-        group_words_shared(nc, w_prompt_grouped[:], w_prompt_raw[:], W_PROMPT_SPLIT)
-        normalise(0)
-        normalise(1)
-        partial_statistics(3)
-        partial_statistics(4)
-        normalise(2)
-        mean_and_variance(3)
-        mean_and_variance(4)
-
         prompt_z_t = banks.tile([P, PACK, P], F32, tag="prompt_z")
-        for t in range(PACK):
-            nc.tensor.transpose(
-                out=prompt_z_t[:, t, :], in_=z[:, 0, t * P : (t + 1) * P], identity=ident_f32[:]
-            )
-        prev_words = prev_raw[:].bitcast(F32)
         prev_t = banks.tile([P, SAMPLES * 2, P], F32, tag="prev")
-        for j in range(SAMPLES * 2):
-            nc.tensor.transpose(
-                out=prev_t[:, j, :], in_=prev_words[:, j * P : (j + 1) * P], identity=ident_f32[:]
-            )
         column_z_t = [
-            banks.tile([P, COLUMNS], F32, tag="column%d" % t, name="column_z_t%d" % t)
-            for t in range(PACK)
+            banks.tile([P, 2, HALF], F32, tag="column%d" % i, name="column_z_t%d" % i)
+            for i in range(4)
         ]
 
         def transpose_columns(r):
+            half, first = divmod((r - 1) * P, HALF)
             for t in range(PACK):
                 nc.tensor.transpose(
-                    out=column_z_t[t][:, (r - 1) * P : r * P],
+                    out=column_z_t[2 * half + t // 2][:, t % 2, first : first + P],
                     in_=z[:, r, t * P : (t + 1) * P],
                     identity=ident_f32[:],
                 )
 
-        transpose_columns(1)
-        transpose_columns(2)
-        warm("vectors", 4)
-        nc.scalar.copy(out=vectors[:], in_=vectors_t[:, 0 : VECTORS * PACK])
+        def copy_vectors(first, last):
+            rows = slice(PACK * first, PACK * last)
+            vectors_t = banks.tile([P, P], BF16, tag="vectors", name="vectors_t%d" % first)
+            nc.tensor.transpose(out=vectors_t[:], in_=vector_rows[:], identity=ident_bf16[:])
+            nc.scalar.copy(out=vectors[:, rows], in_=vectors_t[:, rows])
+
+        def finish_columns(half, t):
+            nc.scalar.activation(
+                out=col_planes[:, t, half * HALF : (half + 1) * HALF],
+                in_=column_z_t[2 * half + t // 2][:, t % 2, :],
+                func=ACT.Identity,
+                scale=vector_column(LN_COL_W, t),
+                bias=vector_column(LN_COL_B, t),
+            )
+
+        warm("vectors", 2)
+        for t in range(PACK):
+            nc.tensor.transpose(
+                out=prompt_t[:, t, :], in_=prompt_raw[:, t * P : (t + 1) * P], identity=ident_bf16[:]
+            )
+        partial_statistics(1)
+        partial_statistics(2)
+        mean_and_variance(1)
+        partial_statistics(3)
+        mean_and_variance(2)
+        partial_statistics(4)
+        mean_and_variance(3)
+        warm("vectors", 2)
+        copy_vectors(LN_PROMPT_W, LN_COL_W)
+        nc.scalar.activation(
+            out=rstd[:, 0:1],
+            in_=row_sums[:, 1:2],
+            func=ACT.Abs_reciprocal_sqrt,
+            scale=1.0 / D**3,
+            bias=eps[:],
+        )
+        load_vector(LN_COL_W, ln_col_w)
+        load_vector(LN_COL_B, ln_col_b)
+        normalise(0)
+        mean_and_variance(4)
+        prev_words = prev_raw[:].bitcast(F32)
+        for j in range(SAMPLES * 2):
+            nc.tensor.transpose(
+                out=prev_t[:, j, :], in_=prev_words[:, j * P : (j + 1) * P], identity=ident_f32[:]
+            )
+
+        def residual_tile(t):
+            nc.scalar.activation(
+                out=residual[:, t, :],
+                in_=prompt_t[:, t, :],
+                func=ACT.Identity,
+                bias=vector_column(B_IMP, t),
+            )
+
+        residual_tile(0)
+        residual_tile(1)
+        reciprocal_std(1, 3)
+        residual_tile(2)
+        residual_tile(3)
+        prev_view = (
+            prev_grouped[:].rearrange("p c t -> p (c t)").bitcast(F32).rearrange("p (n w u) -> p n w u", n=SAMPLES, u=2)
+        )
+        for n in range(SAMPLES):
+            nc.scalar.copy(
+                out=prev_view[:, n, :, :],
+                in_=prev_t[:, 2 * n : 2 * n + 2, :].rearrange("p u w -> p w u"),
+            )
+            if n == 0:
+                reciprocal_std(3, ROW_TILES)
+        for r in range(1, ROW_TILES):
+            normalise(r)
+
+        for t in range(PACK):
+            nc.tensor.transpose(
+                out=prompt_z_t[:, t, :], in_=z[:, 0, t * P : (t + 1) * P], identity=ident_f32[:]
+            )
         for t in range(PACK):
             nc.scalar.activation(
                 out=pn_planes[:, t, :],
@@ -270,50 +309,24 @@ def tile_tromptcell_pa_s_kernel(
                 scale=vector_column(LN_PROMPT_W, t),
                 bias=vector_column(LN_PROMPT_B, t),
             )
-        nc.scalar.copy(
-            out=prev_grouped[:]
-            .rearrange("p c t -> p (c t)")
-            .bitcast(F32)
-            .rearrange("p (n w u) -> p n w u", n=SAMPLES, u=2),
-            in_=prev_t[:].rearrange("p (n u) w -> p n w u", u=2),
-        )
-        reciprocal_std(3, ROW_TILES)
+        transpose_columns(1)
+        transpose_columns(2)
+        group_words_shared(nc, w_prompt_grouped[:], w_prompt_raw[:], W_PROMPT_SPLIT)
+        copy_vectors(LN_COL_W, VECTORS)
         group_words(nc.scalar.copy, pn_grouped[:], pn_planes[:])
-        group_words_shared(nc, w_prev_grouped[:], w_prev_raw[:], W_PREV_SPLIT)
-        normalise(3)
-        normalise(4)
         transpose_columns(3)
         transpose_columns(4)
-        quantise(nc, w_prompt_codes[:], w_prompt_scales[:], w_prompt_grouped[:])
+        warm("vectors", 2)
+        group_words_shared(nc, w_prev_grouped[:], w_prev_raw[:], W_PREV_SPLIT)
+        for t in range(PACK):
+            finish_columns(0, t)
         quantise(nc, prev_codes[:], prev_scales[:], prev_grouped[:])
+        quantise(nc, w_prompt_codes[:], w_prompt_scales[:], w_prompt_grouped[:])
         quantise(nc, pn_codes[:], pn_scales[:], pn_grouped[:])
         quantise(nc, w_prev_codes[:], w_prev_scales[:], w_prev_grouped[:])
         for t in range(PACK):
-            nc.scalar.activation(
-                out=residual[:, t, :],
-                in_=prompt_t[:, t, :],
-                func=ACT.Identity,
-                bias=vector_column(B_IMP, t),
-            )
-
-        for t in range(PACK):
-            if t < PACK - 1:
-                nc.scalar.activation(
-                    out=col_planes[:, t, :],
-                    in_=column_z_t[t][:],
-                    func=ACT.Identity,
-                    scale=vector_column(LN_COL_W, t),
-                    bias=vector_column(LN_COL_B, t),
-                )
-            else:
-                nc.vector.tensor_scalar(
-                    out=col_planes[:, t, :],
-                    in0=column_z_t[t][:],
-                    scalar1=vector_column(LN_COL_W, t),
-                    scalar2=vector_column(LN_COL_B, t),
-                    op0=ALU.mult,
-                    op1=ALU.add,
-                )
+            finish_columns(1, t)
+        group_words_shared(nc, col_grouped[:, 0:HALF, :], col_planes[:, :, 0:HALF], COL0_SPLIT)
 
         def warm_mx(tag, passes):
             unread = banks.tile([P, D], F32, tag=tag, name="unread_mx_" + tag)
@@ -366,34 +379,48 @@ def tile_tromptcell_pa_s_kernel(
                 op=ALU.add,
             )
 
-        for first, last in ((0, HALF), (HALF, COL_SPLIT)):
-            group_words(
-                nc.scalar.copy, col_grouped[:, first:last, :], col_planes[:, :, first:last]
-            )
-        for n in range(SAMPLES):
-            finish_x(n)
-        group_words(nc.vector.tensor_copy, col_grouped[:, COL_SPLIT:, :], col_planes[:, :, COL_SPLIT:])
-        quantise(nc, x_codes[:], x_scales[:], x_grouped[:])
-        pending = []
-        for half in range(2):
+        def quantise_columns(half):
             columns = slice(half * HALF, (half + 1) * HALF)
             quantise(nc, col_codes[:, columns], col_scales[:, columns], col_grouped[:, columns, :])
-            for n, copy in enumerate((nc.scalar.copy, nc.vector.tensor_copy)):
-                prompts = slice(n * P, (n + 1) * P)
-                scores = banks.tile(
-                    [P, HALF], F32, tag="column%d" % (2 * half + n), name="scores%d_%d" % (n, half)
-                )
-                nc.tensor.matmul_mx(
-                    out=scores[:],
-                    lhsT=x_codes[:, prompts].bitcast(FP8X4),
-                    lhsT_scale=x_scales[:, prompts],
-                    rhs=col_codes[:, columns].bitcast(FP8X4),
-                    rhs_scale=col_scales[:, columns],
-                    start=True,
-                    stop=True,
-                )
-                scores_sb = keep.tile([P, HALF], F32, name="scores_sb%d_%d" % (n, half))
-                pending.append((copy, scores_sb, scores, out[n, :, columns]))
-        for copy, scores_sb, scores, destination in pending:
+
+        def quantise_x(n):
+            prompts = slice(n * P, (n + 1) * P)
+            quantise(nc, x_codes[:, prompts], x_scales[:, prompts], x_grouped[:, prompts, :])
+
+        def multiply(n, half):
+            prompts = slice(n * P, (n + 1) * P)
+            columns = slice(half * HALF, (half + 1) * HALF)
+            scores = banks.tile(
+                [P, HALF], F32, tag="column%d" % (2 * half + n), name="scores%d_%d" % (n, half)
+            )
+            nc.tensor.matmul_mx(
+                out=scores[:],
+                lhsT=x_codes[:, prompts].bitcast(FP8X4),
+                lhsT_scale=x_scales[:, prompts],
+                rhs=col_codes[:, columns].bitcast(FP8X4),
+                rhs_scale=col_scales[:, columns],
+                start=True,
+                stop=True,
+            )
+            return scores
+
+        def store(copy, scores, n, half):
+            columns = slice(half * HALF, (half + 1) * HALF)
+            scores_sb = keep.tile([P, HALF], F32, name="scores_sb%d_%d" % (n, half))
             copy(out=scores_sb[:], in_=scores[:])
-            nc.sync.dma_start(out=destination, in_=scores_sb[:])
+            nc.sync.dma_start(out=out[n, :, columns], in_=scores_sb[:])
+
+        group_words_shared(nc, col_grouped[:, HALF:, :], col_planes[:, :, HALF:], COL1_SPLIT)
+        quantise_columns(0)
+        finish_x(0)
+        finish_x(1)
+        quantise_x(0)
+        scores00 = multiply(0, 0)
+        quantise_x(1)
+        scores10 = multiply(1, 0)
+        quantise_columns(1)
+        scores01, scores11 = multiply(0, 1), multiply(1, 1)
+        store(nc.scalar.copy, scores00, 0, 0)
+        store(nc.scalar.copy, scores10, 1, 0)
+        store(nc.scalar.copy, scores01, 0, 1)
+        store(nc.vector.tensor_copy, scores11, 1, 1)

@@ -20,11 +20,8 @@ COLUMN_TILES = COLUMNS // P
 ROW_TILES = 1 + COLUMN_TILES
 EPS = 1e-5
 RUN = 4
-W_PROMPT_SPLIT = 192
-W_PREV_SPLIT = 0
-COL0_SPLIT = 0
-COL1_SPLIT = 192
 HALF = 256
+W_CHUNK = 256
 
 FLOPS = 2 * P * D * D + 2 * SAMPLES * P * D * D + 2 * SAMPLES * P * D * COLUMNS
 
@@ -41,13 +38,6 @@ def group_words(copy, grouped, planes):
         out=grouped.rearrange("p (c i) t -> p c t i", i=RUN),
         in_=planes.rearrange("p t (c i) -> p c t i", i=RUN),
     )
-
-
-def group_words_shared(nc, grouped, planes, split):
-    if split > 0:
-        group_words(nc.scalar.copy, grouped[:, 0:split, :], planes[:, :, 0:split])
-    if split < grouped.shape[1]:
-        group_words(nc.vector.tensor_copy, grouped[:, split:, :], planes[:, :, split:])
 
 
 def quantise(nc, codes, scales, grouped):
@@ -130,22 +120,32 @@ def tile_tromptcell_pa_s_kernel(
                 out=column_raw[:, first:last, :], in_=column_view[:, first:last, :]
             )
 
+        w_prompt_view = W_imp[0:D, :].rearrange("(t p) f -> p t f", p=P)
+
+        def load_w_prompt(chunk):
+            columns = slice(chunk * W_CHUNK, (chunk + 1) * W_CHUNK)
+            nc.sync.dma_start(out=w_prompt_raw[:, :, columns], in_=w_prompt_view[:, :, columns])
+
         load_columns(0, 1)
         nc.sync.dma_start(out=prompt_raw[:], in_=emb_prompt)
         load_columns(1, 2)
-        load_columns(2, COLUMN_TILES)
-        load_vector(LN_PROMPT_W, ln_prompt_w)
-        load_vector(LN_PROMPT_B, ln_prompt_b)
-        load_vector(B_IMP, b_imp)
+        load_columns(2, 3)
+        load_w_prompt(0)
+        load_columns(3, 4)
+        load_w_prompt(1)
         nc.sync.dma_start(
             out=prev_raw[:].rearrange("p (n f) -> p n f", n=SAMPLES),
             in_=prev_cell_out.rearrange("n p f -> p n f"),
         )
-        nc.sync.dma_start(out=w_prompt_raw[:], in_=W_imp[0:D, :].rearrange("(t p) f -> p t f", p=P))
         nc.sync.dma_start(
             out=w_prev_raw[:].rearrange("p (u e) f -> p u e f", u=2),
             in_=W_imp[D : 2 * D, :].rearrange("(u p e) f -> p u e f", u=2, e=2),
         )
+        load_vector(LN_PROMPT_W, ln_prompt_w)
+        load_vector(LN_PROMPT_B, ln_prompt_b)
+        load_vector(B_IMP, b_imp)
+        load_vector(LN_COL_W, ln_col_w)
+        load_vector(LN_COL_B, ln_col_b)
 
         make_identity(nc, ident_bf16[:])
         make_identity(nc, ident_f32[:])
@@ -182,6 +182,7 @@ def tile_tromptcell_pa_s_kernel(
         def vector_column(v, t):
             return vectors[:, PACK * v + t : PACK * v + t + 1]
 
+
         nc.scalar.activation(
             out=unused[:],
             in_=prompt_raw[:],
@@ -200,9 +201,19 @@ def tile_tromptcell_pa_s_kernel(
         nc.scalar.activation(
             out=mean_var[:, 0, 0:1], in_=row_sums[:, 0:1], func=ACT.Copy, scale=-1.0 / D
         )
+        nc.scalar.activation(
+            out=rstd[:, 0:1],
+            in_=row_sums[:, 1:2],
+            func=ACT.Abs_reciprocal_sqrt,
+            scale=1.0 / D**3,
+            bias=eps[:],
+        )
+
+        def group_w_prompt(first, last):
+            group_words(nc.scalar.copy, w_prompt_grouped[:, first:last, :], w_prompt_raw[:, :, first:last])
 
         def warm(tag, passes):
-            unread = banks.tile([P, P], F32, tag=tag, name="unread%d" % passes)
+            unread = banks.tile([P, P], F32, tag=tag, name="unread_" + tag)
             for i in range(passes):
                 nc.tensor.matmul(
                     out=unread[:], lhsT=ident_f32[:], rhs=ident_f32[:], start=True, stop=True
@@ -225,12 +236,6 @@ def tile_tromptcell_pa_s_kernel(
                     identity=ident_f32[:],
                 )
 
-        def copy_vectors(first, last):
-            rows = slice(PACK * first, PACK * last)
-            vectors_t = banks.tile([P, P], BF16, tag="vectors", name="vectors_t%d" % first)
-            nc.tensor.transpose(out=vectors_t[:], in_=vector_rows[:], identity=ident_bf16[:])
-            nc.scalar.copy(out=vectors[:, rows], in_=vectors_t[:, rows])
-
         def finish_columns(half, t):
             nc.scalar.activation(
                 out=col_planes[:, t, half * HALF : (half + 1) * HALF],
@@ -245,6 +250,7 @@ def tile_tromptcell_pa_s_kernel(
             nc.tensor.transpose(
                 out=prompt_t[:, t, :], in_=prompt_raw[:, t * P : (t + 1) * P], identity=ident_bf16[:]
             )
+        warm("vectors", 2)
         partial_statistics(1)
         partial_statistics(2)
         mean_and_variance(1)
@@ -252,17 +258,9 @@ def tile_tromptcell_pa_s_kernel(
         mean_and_variance(2)
         partial_statistics(4)
         mean_and_variance(3)
-        warm("vectors", 2)
-        copy_vectors(LN_PROMPT_W, LN_COL_W)
-        nc.scalar.activation(
-            out=rstd[:, 0:1],
-            in_=row_sums[:, 1:2],
-            func=ACT.Abs_reciprocal_sqrt,
-            scale=1.0 / D**3,
-            bias=eps[:],
-        )
-        load_vector(LN_COL_W, ln_col_w)
-        load_vector(LN_COL_B, ln_col_b)
+        group_w_prompt(0, P)
+        reciprocal_std(1, 3)
+        group_w_prompt(P, HALF)
         normalise(0)
         mean_and_variance(4)
         prev_words = prev_raw[:].bitcast(F32)
@@ -270,37 +268,26 @@ def tile_tromptcell_pa_s_kernel(
             nc.tensor.transpose(
                 out=prev_t[:, j, :], in_=prev_words[:, j * P : (j + 1) * P], identity=ident_f32[:]
             )
-
-        def residual_tile(t):
-            nc.scalar.activation(
-                out=residual[:, t, :],
-                in_=prompt_t[:, t, :],
-                func=ACT.Identity,
-                bias=vector_column(B_IMP, t),
-            )
-
-        residual_tile(0)
-        residual_tile(1)
-        reciprocal_std(1, 3)
-        residual_tile(2)
-        residual_tile(3)
-        prev_view = (
-            prev_grouped[:].rearrange("p c t -> p (c t)").bitcast(F32).rearrange("p (n w u) -> p n w u", n=SAMPLES, u=2)
-        )
-        for n in range(SAMPLES):
-            nc.scalar.copy(
-                out=prev_view[:, n, :, :],
-                in_=prev_t[:, 2 * n : 2 * n + 2, :].rearrange("p u w -> p w u"),
-            )
-            if n == 0:
-                reciprocal_std(3, ROW_TILES)
+        reciprocal_std(3, ROW_TILES)
+        group_w_prompt(HALF, D)
         for r in range(1, ROW_TILES):
             normalise(r)
-
         for t in range(PACK):
             nc.tensor.transpose(
                 out=prompt_z_t[:, t, :], in_=z[:, 0, t * P : (t + 1) * P], identity=ident_f32[:]
             )
+        transpose_columns(1)
+        transpose_columns(2)
+        vectors_t = banks.tile([P, P], BF16, tag="vectors")
+        nc.tensor.transpose(out=vectors_t[:], in_=vector_rows[:], identity=ident_bf16[:])
+        nc.scalar.copy(out=vectors[:], in_=vectors_t[:, 0 : VECTORS * PACK])
+        nc.scalar.copy(
+            out=prev_grouped[:]
+            .rearrange("p c t -> p (c t)")
+            .bitcast(F32)
+            .rearrange("p (n w u) -> p n w u", n=SAMPLES, u=2),
+            in_=prev_t[:].rearrange("p (n u) w -> p n w u", u=2),
+        )
         for t in range(PACK):
             nc.scalar.activation(
                 out=pn_planes[:, t, :],
@@ -309,24 +296,31 @@ def tile_tromptcell_pa_s_kernel(
                 scale=vector_column(LN_PROMPT_W, t),
                 bias=vector_column(LN_PROMPT_B, t),
             )
-        transpose_columns(1)
-        transpose_columns(2)
-        group_words_shared(nc, w_prompt_grouped[:], w_prompt_raw[:], W_PROMPT_SPLIT)
-        copy_vectors(LN_COL_W, VECTORS)
-        group_words(nc.scalar.copy, pn_grouped[:], pn_planes[:])
+        warm("vectors", 2)
         transpose_columns(3)
         transpose_columns(4)
         warm("vectors", 2)
-        group_words_shared(nc, w_prev_grouped[:], w_prev_raw[:], W_PREV_SPLIT)
-        for t in range(PACK):
-            finish_columns(0, t)
-        quantise(nc, prev_codes[:], prev_scales[:], prev_grouped[:])
+        finish_columns(0, 0)
+        group_words(nc.scalar.copy, pn_grouped[:], pn_planes[:])
+        group_words(nc.vector.tensor_copy, w_prev_grouped[:], w_prev_raw[:])
         quantise(nc, w_prompt_codes[:], w_prompt_scales[:], w_prompt_grouped[:])
-        quantise(nc, pn_codes[:], pn_scales[:], pn_grouped[:])
+        quantise(nc, prev_codes[:], prev_scales[:], prev_grouped[:])
         quantise(nc, w_prev_codes[:], w_prev_scales[:], w_prev_grouped[:])
-        for t in range(PACK):
+        quantise(nc, pn_codes[:], pn_scales[:], pn_grouped[:])
+
+        nc.vector.tensor_tensor(
+            out=residual[:],
+            in0=prompt_t[:],
+            in1=vectors[:, PACK * B_IMP : PACK * (B_IMP + 1)].unsqueeze(2).to_broadcast([P, PACK, P]),
+            op=ALU.add,
+        )
+        for t in range(1, PACK):
+            finish_columns(0, t)
+        finish_columns(1, 0)
+        group_words(nc.vector.tensor_copy, col_grouped[:, P:HALF, :], col_planes[:, :, P:HALF])
+        group_words(nc.scalar.copy, col_grouped[:, 0:P, :], col_planes[:, :, 0:P])
+        for t in range(1, PACK):
             finish_columns(1, t)
-        group_words_shared(nc, col_grouped[:, 0:HALF, :], col_planes[:, :, 0:HALF], COL0_SPLIT)
 
         def warm_mx(tag, passes):
             unread = banks.tile([P, D], F32, tag=tag, name="unread_mx_" + tag)
@@ -341,7 +335,7 @@ def tile_tromptcell_pa_s_kernel(
                     stop=True,
                 )
 
-        warm_mx("prev", 1)
+        warm_mx("prev", 2)
         x_t = [
             banks.tile([P, PACK, P], F32, tag=tag, name="x_t%d" % n)
             for n, tag in enumerate(("vectors", "prompt_z"))
@@ -379,20 +373,18 @@ def tile_tromptcell_pa_s_kernel(
                 op=ALU.add,
             )
 
-        def quantise_columns(half):
-            columns = slice(half * HALF, (half + 1) * HALF)
+        def quantise_columns(first, last):
+            columns = slice(first, last)
             quantise(nc, col_codes[:, columns], col_scales[:, columns], col_grouped[:, columns, :])
 
         def quantise_x(n):
             prompts = slice(n * P, (n + 1) * P)
             quantise(nc, x_codes[:, prompts], x_scales[:, prompts], x_grouped[:, prompts, :])
 
-        def multiply(n, half):
+        def multiply(n, first, last, tag):
             prompts = slice(n * P, (n + 1) * P)
-            columns = slice(half * HALF, (half + 1) * HALF)
-            scores = banks.tile(
-                [P, HALF], F32, tag="column%d" % (2 * half + n), name="scores%d_%d" % (n, half)
-            )
+            columns = slice(first, last)
+            scores = banks.tile([P, last - first], F32, tag=tag, name="scores%d_%d" % (n, first))
             nc.tensor.matmul_mx(
                 out=scores[:],
                 lhsT=x_codes[:, prompts].bitcast(FP8X4),
@@ -404,23 +396,29 @@ def tile_tromptcell_pa_s_kernel(
             )
             return scores
 
-        def store(copy, scores, n, half):
-            columns = slice(half * HALF, (half + 1) * HALF)
-            scores_sb = keep.tile([P, HALF], F32, name="scores_sb%d_%d" % (n, half))
+        def store(copy, scores, n, first, last):
+            scores_sb = keep.tile([P, last - first], F32, name="scores_sb%d_%d" % (n, first))
             copy(out=scores_sb[:], in_=scores[:])
-            nc.sync.dma_start(out=out[n, :, columns], in_=scores_sb[:])
+            nc.sync.dma_start(out=out[n, :, first:last], in_=scores_sb[:])
 
-        group_words_shared(nc, col_grouped[:, HALF:, :], col_planes[:, :, HALF:], COL1_SPLIT)
-        quantise_columns(0)
+        A, B, C = (0, 256), (256, 384), (384, 512)
+        S, V = nc.scalar.copy, nc.vector.tensor_copy
         finish_x(0)
-        finish_x(1)
+        quantise_columns(*A)
         quantise_x(0)
-        scores00 = multiply(0, 0)
+        a0 = multiply(0, *A, "column0")
+        finish_x(1)
+        group_words(S, col_grouped[:, B[0] : B[1], :], col_planes[:, :, B[0] : B[1]])
+        store(S, a0, 0, *A)
         quantise_x(1)
-        scores10 = multiply(1, 0)
-        quantise_columns(1)
-        scores01, scores11 = multiply(0, 1), multiply(1, 1)
-        store(nc.scalar.copy, scores00, 0, 0)
-        store(nc.scalar.copy, scores10, 1, 0)
-        store(nc.scalar.copy, scores01, 0, 1)
-        store(nc.vector.tensor_copy, scores11, 1, 1)
+        a1 = multiply(1, *A, "column1")
+        group_words(V, col_grouped[:, C[0] : C[1], :], col_planes[:, :, C[0] : C[1]])
+        quantise_columns(*B)
+        b0, b1 = multiply(0, *B, "prev"), multiply(1, *B, "vectors")
+        quantise_columns(*C)
+        c0, c1 = multiply(0, *C, "column2"), multiply(1, *C, "column3")
+        store(S, a1, 1, *A)
+        store(V, b1, 1, *B)
+        store(S, b0, 0, *B)
+        store(V, c1, 1, *C)
+        store(S, c0, 0, *C)

@@ -21,7 +21,7 @@ ROW_TILES = 1 + COLUMN_TILES
 EPS = 1e-5
 RUN = 4
 HALF = 256
-W_CHUNK = 256
+W_PROMPT_SPLIT = 448
 
 FLOPS = 2 * P * D * D + 2 * SAMPLES * P * D * D + 2 * SAMPLES * P * D * COLUMNS
 
@@ -120,19 +120,16 @@ def tile_tromptcell_pa_s_kernel(
                 out=column_raw[:, first:last, :], in_=column_view[:, first:last, :]
             )
 
-        w_prompt_view = W_imp[0:D, :].rearrange("(t p) f -> p t f", p=P)
-
-        def load_w_prompt(chunk):
-            columns = slice(chunk * W_CHUNK, (chunk + 1) * W_CHUNK)
-            nc.sync.dma_start(out=w_prompt_raw[:, :, columns], in_=w_prompt_view[:, :, columns])
-
         load_columns(0, 1)
         nc.sync.dma_start(out=prompt_raw[:], in_=emb_prompt)
         load_columns(1, 2)
-        load_columns(2, 3)
-        load_w_prompt(0)
-        load_columns(3, 4)
-        load_w_prompt(1)
+        load_columns(2, COLUMN_TILES)
+        nc.sync.dma_start(out=w_prompt_raw[:], in_=W_imp[0:D, :].rearrange("(t p) f -> p t f", p=P))
+        load_vector(LN_PROMPT_W, ln_prompt_w)
+        load_vector(LN_PROMPT_B, ln_prompt_b)
+        load_vector(B_IMP, b_imp)
+        load_vector(LN_COL_W, ln_col_w)
+        load_vector(LN_COL_B, ln_col_b)
         nc.sync.dma_start(
             out=prev_raw[:].rearrange("p (n f) -> p n f", n=SAMPLES),
             in_=prev_cell_out.rearrange("n p f -> p n f"),
@@ -141,11 +138,6 @@ def tile_tromptcell_pa_s_kernel(
             out=w_prev_raw[:].rearrange("p (u e) f -> p u e f", u=2),
             in_=W_imp[D : 2 * D, :].rearrange("(u p e) f -> p u e f", u=2, e=2),
         )
-        load_vector(LN_PROMPT_W, ln_prompt_w)
-        load_vector(LN_PROMPT_B, ln_prompt_b)
-        load_vector(B_IMP, b_imp)
-        load_vector(LN_COL_W, ln_col_w)
-        load_vector(LN_COL_B, ln_col_b)
 
         make_identity(nc, ident_bf16[:])
         make_identity(nc, ident_f32[:])
@@ -251,6 +243,8 @@ def tile_tromptcell_pa_s_kernel(
                 out=prompt_t[:, t, :], in_=prompt_raw[:, t * P : (t + 1) * P], identity=ident_bf16[:]
             )
         warm("vectors", 2)
+        vectors_t = banks.tile([P, P], BF16, tag="vectors")
+        nc.tensor.transpose(out=vectors_t[:], in_=vector_rows[:], identity=ident_bf16[:])
         partial_statistics(1)
         partial_statistics(2)
         mean_and_variance(1)
@@ -258,9 +252,8 @@ def tile_tromptcell_pa_s_kernel(
         mean_and_variance(2)
         partial_statistics(4)
         mean_and_variance(3)
-        group_w_prompt(0, P)
         reciprocal_std(1, 3)
-        group_w_prompt(P, HALF)
+        group_w_prompt(0, P)
         normalise(0)
         mean_and_variance(4)
         prev_words = prev_raw[:].bitcast(F32)
@@ -268,8 +261,10 @@ def tile_tromptcell_pa_s_kernel(
             nc.tensor.transpose(
                 out=prev_t[:, j, :], in_=prev_words[:, j * P : (j + 1) * P], identity=ident_f32[:]
             )
+        warm("vectors", 1)
         reciprocal_std(3, ROW_TILES)
-        group_w_prompt(HALF, D)
+        nc.scalar.copy(out=vectors[:], in_=vectors_t[:, 0 : VECTORS * PACK])
+        group_w_prompt(P, W_PROMPT_SPLIT)
         for r in range(1, ROW_TILES):
             normalise(r)
         for t in range(PACK):
@@ -277,10 +272,8 @@ def tile_tromptcell_pa_s_kernel(
                 out=prompt_z_t[:, t, :], in_=z[:, 0, t * P : (t + 1) * P], identity=ident_f32[:]
             )
         transpose_columns(1)
+        warm("vectors", 1)
         transpose_columns(2)
-        vectors_t = banks.tile([P, P], BF16, tag="vectors")
-        nc.tensor.transpose(out=vectors_t[:], in_=vector_rows[:], identity=ident_bf16[:])
-        nc.scalar.copy(out=vectors[:], in_=vectors_t[:, 0 : VECTORS * PACK])
         nc.scalar.copy(
             out=prev_grouped[:]
             .rearrange("p c t -> p (c t)")
@@ -296,12 +289,16 @@ def tile_tromptcell_pa_s_kernel(
                 scale=vector_column(LN_PROMPT_W, t),
                 bias=vector_column(LN_PROMPT_B, t),
             )
-        warm("vectors", 2)
+        warm("vectors", 1)
         transpose_columns(3)
         transpose_columns(4)
-        warm("vectors", 2)
-        finish_columns(0, 0)
+        warm("vectors", 1)
         group_words(nc.scalar.copy, pn_grouped[:], pn_planes[:])
+        group_words(
+            nc.vector.tensor_copy,
+            w_prompt_grouped[:, W_PROMPT_SPLIT:, :],
+            w_prompt_raw[:, :, W_PROMPT_SPLIT:],
+        )
         group_words(nc.vector.tensor_copy, w_prev_grouped[:], w_prev_raw[:])
         quantise(nc, w_prompt_codes[:], w_prompt_scales[:], w_prompt_grouped[:])
         quantise(nc, prev_codes[:], prev_scales[:], prev_grouped[:])
@@ -314,11 +311,11 @@ def tile_tromptcell_pa_s_kernel(
             in1=vectors[:, PACK * B_IMP : PACK * (B_IMP + 1)].unsqueeze(2).to_broadcast([P, PACK, P]),
             op=ALU.add,
         )
-        for t in range(1, PACK):
+        for t in range(PACK):
             finish_columns(0, t)
         finish_columns(1, 0)
-        group_words(nc.vector.tensor_copy, col_grouped[:, P:HALF, :], col_planes[:, :, P:HALF])
-        group_words(nc.scalar.copy, col_grouped[:, 0:P, :], col_planes[:, :, 0:P])
+        group_words(nc.vector.tensor_copy, col_grouped[:, P : HALF, :], col_planes[:, :, P : HALF])
+        group_words(nc.scalar.copy, col_grouped[:, 0 : P, :], col_planes[:, :, 0 : P])
         for t in range(1, PACK):
             finish_columns(1, t)
 

@@ -21,7 +21,8 @@ ROW_TILES = 1 + COLUMN_TILES
 EPS = 1e-5
 RUN = 4
 HALF = 256
-W_PROMPT_SPLIT = 448
+W_GPSIMD = 128
+W_PREV_SPLIT = 64
 
 FLOPS = 2 * P * D * D + 2 * SAMPLES * P * D * D + 2 * SAMPLES * P * D * COLUMNS
 
@@ -37,6 +38,17 @@ def group_words(copy, grouped, planes):
     copy(
         out=grouped.rearrange("p (c i) t -> p c t i", i=RUN),
         in_=planes.rearrange("p t (c i) -> p c t i", i=RUN),
+    )
+
+
+def group_words_gpsimd(nc, grouped, planes):
+    nc.gpsimd.tensor_scalar(
+        out=grouped,
+        in0=planes.rearrange("p t c -> p c t"),
+        scalar1=1.0,
+        scalar2=0.0,
+        op0=ALU.mult,
+        op1=ALU.add,
     )
 
 
@@ -120,16 +132,18 @@ def tile_tromptcell_pa_s_kernel(
                 out=column_raw[:, first:last, :], in_=column_view[:, first:last, :]
             )
 
+        w_prompt_view = W_imp[0:D, :].rearrange("(t p) f -> p t f", p=P)
+
+        def load_w_prompt(first, last):
+            nc.sync.dma_start(out=w_prompt_raw[:, :, first:last], in_=w_prompt_view[:, :, first:last])
+
         load_columns(0, 1)
         nc.sync.dma_start(out=prompt_raw[:], in_=emb_prompt)
         load_columns(1, 2)
-        load_columns(2, COLUMN_TILES)
-        nc.sync.dma_start(out=w_prompt_raw[:], in_=W_imp[0:D, :].rearrange("(t p) f -> p t f", p=P))
-        load_vector(LN_PROMPT_W, ln_prompt_w)
-        load_vector(LN_PROMPT_B, ln_prompt_b)
-        load_vector(B_IMP, b_imp)
-        load_vector(LN_COL_W, ln_col_w)
-        load_vector(LN_COL_B, ln_col_b)
+        load_w_prompt(0, HALF)
+        load_columns(2, 3)
+        load_columns(3, 4)
+        load_w_prompt(HALF, D)
         nc.sync.dma_start(
             out=prev_raw[:].rearrange("p (n f) -> p n f", n=SAMPLES),
             in_=prev_cell_out.rearrange("n p f -> p n f"),
@@ -138,6 +152,11 @@ def tile_tromptcell_pa_s_kernel(
             out=w_prev_raw[:].rearrange("p (u e) f -> p u e f", u=2),
             in_=W_imp[D : 2 * D, :].rearrange("(u p e) f -> p u e f", u=2, e=2),
         )
+        load_vector(LN_PROMPT_W, ln_prompt_w)
+        load_vector(LN_PROMPT_B, ln_prompt_b)
+        load_vector(B_IMP, b_imp)
+        load_vector(LN_COL_W, ln_col_w)
+        load_vector(LN_COL_B, ln_col_b)
 
         make_identity(nc, ident_bf16[:])
         make_identity(nc, ident_f32[:])
@@ -214,10 +233,13 @@ def tile_tromptcell_pa_s_kernel(
         prompt_t = banks.tile([P, PACK, P], BF16, tag="prompt")
         prompt_z_t = banks.tile([P, PACK, P], F32, tag="prompt_z")
         prev_t = banks.tile([P, SAMPLES * 2, P], F32, tag="prev")
-        column_z_t = [
-            banks.tile([P, 2, HALF], F32, tag="column%d" % i, name="column_z_t%d" % i)
-            for i in range(4)
-        ]
+        def column_banks(half):
+            return [
+                banks.tile([P, 2, HALF], F32, tag="column%d" % i, name="column_z_t%d" % i)
+                for i in (2 * half, 2 * half + 1)
+            ]
+
+        column_z_t = column_banks(0)
 
         def transpose_columns(r):
             half, first = divmod((r - 1) * P, HALF)
@@ -237,23 +259,23 @@ def tile_tromptcell_pa_s_kernel(
                 bias=vector_column(LN_COL_B, t),
             )
 
-        warm("vectors", 2)
+        warm("column3", 2)
         for t in range(PACK):
             nc.tensor.transpose(
                 out=prompt_t[:, t, :], in_=prompt_raw[:, t * P : (t + 1) * P], identity=ident_bf16[:]
             )
-        warm("vectors", 2)
-        vectors_t = banks.tile([P, P], BF16, tag="vectors")
-        nc.tensor.transpose(out=vectors_t[:], in_=vector_rows[:], identity=ident_bf16[:])
+        warm("column3", 2)
         partial_statistics(1)
+        group_words_gpsimd(nc, w_prompt_grouped[:, 0:W_GPSIMD, :], w_prompt_raw[:, :, 0:W_GPSIMD])
         partial_statistics(2)
         mean_and_variance(1)
         partial_statistics(3)
         mean_and_variance(2)
         partial_statistics(4)
         mean_and_variance(3)
+        group_w_prompt(W_GPSIMD, W_GPSIMD + 64)
         reciprocal_std(1, 3)
-        group_w_prompt(0, P)
+        group_w_prompt(W_GPSIMD + 64, 384)
         normalise(0)
         mean_and_variance(4)
         prev_words = prev_raw[:].bitcast(F32)
@@ -261,18 +283,19 @@ def tile_tromptcell_pa_s_kernel(
             nc.tensor.transpose(
                 out=prev_t[:, j, :], in_=prev_words[:, j * P : (j + 1) * P], identity=ident_f32[:]
             )
-        warm("vectors", 1)
+        warm("column3", 1)
         reciprocal_std(3, ROW_TILES)
-        nc.scalar.copy(out=vectors[:], in_=vectors_t[:, 0 : VECTORS * PACK])
-        group_w_prompt(P, W_PROMPT_SPLIT)
+        group_w_prompt(384, D)
         for r in range(1, ROW_TILES):
             normalise(r)
         for t in range(PACK):
             nc.tensor.transpose(
                 out=prompt_z_t[:, t, :], in_=z[:, 0, t * P : (t + 1) * P], identity=ident_f32[:]
             )
+        vectors_t = banks.tile([P, P], BF16, tag="vectors")
+        nc.tensor.transpose(out=vectors_t[:], in_=vector_rows[:], identity=ident_bf16[:])
         transpose_columns(1)
-        warm("vectors", 1)
+        warm("column3", 1)
         transpose_columns(2)
         nc.scalar.copy(
             out=prev_grouped[:]
@@ -281,6 +304,8 @@ def tile_tromptcell_pa_s_kernel(
             .rearrange("p (n w u) -> p n w u", n=SAMPLES, u=2),
             in_=prev_t[:].rearrange("p (n u) w -> p n w u", u=2),
         )
+        group_words(nc.scalar.copy, w_prev_grouped[:, 0:W_PREV_SPLIT, :], w_prev_raw[:, :, 0:W_PREV_SPLIT])
+        nc.scalar.copy(out=vectors[:], in_=vectors_t[:, 0 : VECTORS * PACK])
         for t in range(PACK):
             nc.scalar.activation(
                 out=pn_planes[:, t, :],
@@ -289,17 +314,13 @@ def tile_tromptcell_pa_s_kernel(
                 scale=vector_column(LN_PROMPT_W, t),
                 bias=vector_column(LN_PROMPT_B, t),
             )
-        warm("vectors", 1)
+        warm("column3", 1)
+        column_z_t = column_z_t + column_banks(1)
         transpose_columns(3)
         transpose_columns(4)
         warm("vectors", 1)
         group_words(nc.scalar.copy, pn_grouped[:], pn_planes[:])
-        group_words(
-            nc.vector.tensor_copy,
-            w_prompt_grouped[:, W_PROMPT_SPLIT:, :],
-            w_prompt_raw[:, :, W_PROMPT_SPLIT:],
-        )
-        group_words(nc.vector.tensor_copy, w_prev_grouped[:], w_prev_raw[:])
+        group_words(nc.vector.tensor_copy, w_prev_grouped[:, W_PREV_SPLIT:, :], w_prev_raw[:, :, W_PREV_SPLIT:])
         quantise(nc, w_prompt_codes[:], w_prompt_scales[:], w_prompt_grouped[:])
         quantise(nc, prev_codes[:], prev_scales[:], prev_grouped[:])
         quantise(nc, w_prev_codes[:], w_prev_scales[:], w_prev_grouped[:])
@@ -401,21 +422,21 @@ def tile_tromptcell_pa_s_kernel(
         A, B, C = (0, 256), (256, 384), (384, 512)
         S, V = nc.scalar.copy, nc.vector.tensor_copy
         finish_x(0)
+        finish_x(1)
+        group_words(S, col_grouped[:, B[0] : B[1], :], col_planes[:, :, B[0] : B[1]])
         quantise_columns(*A)
         quantise_x(0)
         a0 = multiply(0, *A, "column0")
-        finish_x(1)
-        group_words(S, col_grouped[:, B[0] : B[1], :], col_planes[:, :, B[0] : B[1]])
-        store(S, a0, 0, *A)
         quantise_x(1)
         a1 = multiply(1, *A, "column1")
         group_words(V, col_grouped[:, C[0] : C[1], :], col_planes[:, :, C[0] : C[1]])
+        store(S, a0, 0, *A)
         quantise_columns(*B)
         b0, b1 = multiply(0, *B, "prev"), multiply(1, *B, "vectors")
         quantise_columns(*C)
         c0, c1 = multiply(0, *C, "column2"), multiply(1, *C, "column3")
-        store(S, a1, 1, *A)
-        store(V, b1, 1, *B)
+        store(V, a1, 1, *A)
         store(S, b0, 0, *B)
-        store(V, c1, 1, *C)
+        store(V, b1, 1, *B)
         store(S, c0, 0, *C)
+        store(V, c1, 1, *C)

@@ -21,7 +21,7 @@ ROW_TILES = 1 + COLUMN_TILES
 EPS = 1e-5
 RUN = 4
 HALF = 256
-W_GPSIMD = 128
+W_PROMPT_SPLIT = 320
 W_PREV_SPLIT = 64
 
 FLOPS = 2 * P * D * D + 2 * SAMPLES * P * D * D + 2 * SAMPLES * P * D * COLUMNS
@@ -38,17 +38,6 @@ def group_words(copy, grouped, planes):
     copy(
         out=grouped.rearrange("p (c i) t -> p c t i", i=RUN),
         in_=planes.rearrange("p t (c i) -> p c t i", i=RUN),
-    )
-
-
-def group_words_gpsimd(nc, grouped, planes):
-    nc.gpsimd.tensor_scalar(
-        out=grouped,
-        in0=planes.rearrange("p t c -> p c t"),
-        scalar1=1.0,
-        scalar2=0.0,
-        op0=ALU.mult,
-        op1=ALU.add,
     )
 
 
@@ -132,31 +121,24 @@ def tile_tromptcell_pa_s_kernel(
                 out=column_raw[:, first:last, :], in_=column_view[:, first:last, :]
             )
 
-        w_prompt_view = W_imp[0:D, :].rearrange("(t p) f -> p t f", p=P)
-
-        def load_w_prompt(first, last):
-            nc.sync.dma_start(out=w_prompt_raw[:, :, first:last], in_=w_prompt_view[:, :, first:last])
-
         load_columns(0, 1)
         nc.sync.dma_start(out=prompt_raw[:], in_=emb_prompt)
         load_columns(1, 2)
-        load_w_prompt(0, HALF)
-        load_columns(2, 3)
-        load_columns(3, 4)
-        load_w_prompt(HALF, D)
-        nc.sync.dma_start(
-            out=prev_raw[:].rearrange("p (n f) -> p n f", n=SAMPLES),
-            in_=prev_cell_out.rearrange("n p f -> p n f"),
-        )
-        nc.sync.dma_start(
-            out=w_prev_raw[:].rearrange("p (u e) f -> p u e f", u=2),
-            in_=W_imp[D : 2 * D, :].rearrange("(u p e) f -> p u e f", u=2, e=2),
-        )
+        load_columns(2, COLUMN_TILES)
+        nc.sync.dma_start(out=w_prompt_raw[:], in_=W_imp[0:D, :].rearrange("(t p) f -> p t f", p=P))
         load_vector(LN_PROMPT_W, ln_prompt_w)
         load_vector(LN_PROMPT_B, ln_prompt_b)
         load_vector(B_IMP, b_imp)
         load_vector(LN_COL_W, ln_col_w)
         load_vector(LN_COL_B, ln_col_b)
+        nc.sync.dma_start(
+            out=w_prev_raw[:].rearrange("p (u e) f -> p u e f", u=2),
+            in_=W_imp[D : 2 * D, :].rearrange("(u p e) f -> p u e f", u=2, e=2),
+        )
+        nc.sync.dma_start(
+            out=prev_raw[:].rearrange("p (n f) -> p n f", n=SAMPLES),
+            in_=prev_cell_out.rearrange("n p f -> p n f"),
+        )
 
         make_identity(nc, ident_bf16[:])
         make_identity(nc, ident_f32[:])
@@ -233,13 +215,10 @@ def tile_tromptcell_pa_s_kernel(
         prompt_t = banks.tile([P, PACK, P], BF16, tag="prompt")
         prompt_z_t = banks.tile([P, PACK, P], F32, tag="prompt_z")
         prev_t = banks.tile([P, SAMPLES * 2, P], F32, tag="prev")
-        def column_banks(half):
-            return [
-                banks.tile([P, 2, HALF], F32, tag="column%d" % i, name="column_z_t%d" % i)
-                for i in (2 * half, 2 * half + 1)
-            ]
-
-        column_z_t = column_banks(0)
+        column_z_t = [
+            banks.tile([P, 2, HALF], F32, tag="column%d" % i, name="column_z_t%d" % i)
+            for i in range(4)
+        ]
 
         def transpose_columns(r):
             half, first = divmod((r - 1) * P, HALF)
@@ -250,62 +229,68 @@ def tile_tromptcell_pa_s_kernel(
                     identity=ident_f32[:],
                 )
 
-        def finish_columns(half, t):
-            nc.scalar.activation(
-                out=col_planes[:, t, half * HALF : (half + 1) * HALF],
-                in_=column_z_t[2 * half + t // 2][:, t % 2, :],
-                func=ACT.Identity,
-                scale=vector_column(LN_COL_W, t),
-                bias=vector_column(LN_COL_B, t),
-            )
+        def finish_columns(half, t, by_vector=False):
+            planes = col_planes[:, t, half * HALF : (half + 1) * HALF]
+            transposed = column_z_t[2 * half + t // 2][:, t % 2, :]
+            gain, bias = vector_column(LN_COL_W, t), vector_column(LN_COL_B, t)
+            if by_vector:
+                nc.vector.tensor_scalar(
+                    out=planes, in0=transposed, scalar1=gain, scalar2=bias, op0=ALU.mult, op1=ALU.add
+                )
+            else:
+                nc.scalar.activation(
+                    out=planes, in_=transposed, func=ACT.Identity, scale=gain, bias=bias
+                )
 
-        warm("column3", 2)
+        warm("vectors", 2)
         for t in range(PACK):
             nc.tensor.transpose(
                 out=prompt_t[:, t, :], in_=prompt_raw[:, t * P : (t + 1) * P], identity=ident_bf16[:]
             )
-        warm("column3", 2)
+        warm("vectors", 2)
+        vectors_t = banks.tile([P, P], BF16, tag="vectors")
+        nc.tensor.transpose(out=vectors_t[:], in_=vector_rows[:], identity=ident_bf16[:])
         partial_statistics(1)
-        group_words_gpsimd(nc, w_prompt_grouped[:, 0:W_GPSIMD, :], w_prompt_raw[:, :, 0:W_GPSIMD])
         partial_statistics(2)
         mean_and_variance(1)
         partial_statistics(3)
         mean_and_variance(2)
         partial_statistics(4)
         mean_and_variance(3)
-        group_w_prompt(W_GPSIMD, W_GPSIMD + 64)
         reciprocal_std(1, 3)
-        group_w_prompt(W_GPSIMD + 64, 384)
+        group_w_prompt(0, P)
         normalise(0)
         mean_and_variance(4)
-        prev_words = prev_raw[:].bitcast(F32)
-        for j in range(SAMPLES * 2):
-            nc.tensor.transpose(
-                out=prev_t[:, j, :], in_=prev_words[:, j * P : (j + 1) * P], identity=ident_f32[:]
-            )
-        warm("column3", 1)
+        def transpose_prev():
+            prev_words = prev_raw[:].bitcast(F32)
+            for j in range(SAMPLES * 2):
+                nc.tensor.transpose(
+                    out=prev_t[:, j, :], in_=prev_words[:, j * P : (j + 1) * P], identity=ident_f32[:]
+                )
+            warm("vectors", 1)
+
         reciprocal_std(3, ROW_TILES)
-        group_w_prompt(384, D)
+        nc.scalar.copy(out=vectors[:], in_=vectors_t[:, 0 : VECTORS * PACK])
+        group_w_prompt(P, W_PROMPT_SPLIT)
         for r in range(1, ROW_TILES):
             normalise(r)
         for t in range(PACK):
             nc.tensor.transpose(
                 out=prompt_z_t[:, t, :], in_=z[:, 0, t * P : (t + 1) * P], identity=ident_f32[:]
             )
-        vectors_t = banks.tile([P, P], BF16, tag="vectors")
-        nc.tensor.transpose(out=vectors_t[:], in_=vector_rows[:], identity=ident_bf16[:])
         transpose_columns(1)
-        warm("column3", 1)
+        warm("vectors", 1)
         transpose_columns(2)
-        nc.scalar.copy(
-            out=prev_grouped[:]
-            .rearrange("p c t -> p (c t)")
-            .bitcast(F32)
-            .rearrange("p (n w u) -> p n w u", n=SAMPLES, u=2),
-            in_=prev_t[:].rearrange("p (n u) w -> p n w u", u=2),
-        )
-        group_words(nc.scalar.copy, w_prev_grouped[:, 0:W_PREV_SPLIT, :], w_prev_raw[:, :, 0:W_PREV_SPLIT])
-        nc.scalar.copy(out=vectors[:], in_=vectors_t[:, 0 : VECTORS * PACK])
+        transpose_prev()
+        def copy_prev():
+            nc.scalar.copy(
+                out=prev_grouped[:]
+                .rearrange("p c t -> p (c t)")
+                .bitcast(F32)
+                .rearrange("p (n w u) -> p n w u", n=SAMPLES, u=2),
+                in_=prev_t[:].rearrange("p (n u) w -> p n w u", u=2),
+            )
+
         for t in range(PACK):
             nc.scalar.activation(
                 out=pn_planes[:, t, :],
@@ -314,17 +299,19 @@ def tile_tromptcell_pa_s_kernel(
                 scale=vector_column(LN_PROMPT_W, t),
                 bias=vector_column(LN_PROMPT_B, t),
             )
-        warm("column3", 1)
-        column_z_t = column_z_t + column_banks(1)
+        warm("vectors", 1)
         transpose_columns(3)
         transpose_columns(4)
         warm("vectors", 1)
+        group_words(nc.scalar.copy, w_prev_grouped[:, 0:W_PREV_SPLIT, :], w_prev_raw[:, :, 0:W_PREV_SPLIT])
         group_words(nc.scalar.copy, pn_grouped[:], pn_planes[:])
+        copy_prev()
+        group_words(nc.vector.tensor_copy, w_prompt_grouped[:, W_PROMPT_SPLIT:, :], w_prompt_raw[:, :, W_PROMPT_SPLIT:])
         group_words(nc.vector.tensor_copy, w_prev_grouped[:, W_PREV_SPLIT:, :], w_prev_raw[:, :, W_PREV_SPLIT:])
         quantise(nc, w_prompt_codes[:], w_prompt_scales[:], w_prompt_grouped[:])
-        quantise(nc, prev_codes[:], prev_scales[:], prev_grouped[:])
         quantise(nc, w_prev_codes[:], w_prev_scales[:], w_prev_grouped[:])
         quantise(nc, pn_codes[:], pn_scales[:], pn_grouped[:])
+        quantise(nc, prev_codes[:], prev_scales[:], prev_grouped[:])
 
         nc.vector.tensor_tensor(
             out=residual[:],

@@ -21,8 +21,9 @@ ROW_TILES = 1 + COLUMN_TILES
 EPS = 1e-5
 RUN = 4
 HALF = 256
-W_PROMPT_SPLIT = 320
-W_PREV_SPLIT = 64
+W_PROMPT_SPLIT = 352
+W_PREV_SPLIT = 32
+COL_SPLIT = 64
 
 FLOPS = 2 * P * D * D + 2 * SAMPLES * P * D * D + 2 * SAMPLES * P * D * COLUMNS
 
@@ -215,10 +216,13 @@ def tile_tromptcell_pa_s_kernel(
         prompt_t = banks.tile([P, PACK, P], BF16, tag="prompt")
         prompt_z_t = banks.tile([P, PACK, P], F32, tag="prompt_z")
         prev_t = banks.tile([P, SAMPLES * 2, P], F32, tag="prev")
-        column_z_t = [
-            banks.tile([P, 2, HALF], F32, tag="column%d" % i, name="column_z_t%d" % i)
-            for i in range(4)
-        ]
+        def column_banks(half):
+            return [
+                banks.tile([P, 2, HALF], F32, tag="column%d" % i, name="column_z_t%d" % i)
+                for i in (2 * half, 2 * half + 1)
+            ]
+
+        column_z_t = column_banks(0)
 
         def transpose_columns(r):
             half, first = divmod((r - 1) * P, HALF)
@@ -229,25 +233,21 @@ def tile_tromptcell_pa_s_kernel(
                     identity=ident_f32[:],
                 )
 
-        def finish_columns(half, t, by_vector=False):
-            planes = col_planes[:, t, half * HALF : (half + 1) * HALF]
-            transposed = column_z_t[2 * half + t // 2][:, t % 2, :]
-            gain, bias = vector_column(LN_COL_W, t), vector_column(LN_COL_B, t)
-            if by_vector:
-                nc.vector.tensor_scalar(
-                    out=planes, in0=transposed, scalar1=gain, scalar2=bias, op0=ALU.mult, op1=ALU.add
-                )
-            else:
-                nc.scalar.activation(
-                    out=planes, in_=transposed, func=ACT.Identity, scale=gain, bias=bias
-                )
+        def finish_columns(half, t):
+            nc.scalar.activation(
+                out=col_planes[:, t, half * HALF : (half + 1) * HALF],
+                in_=column_z_t[2 * half + t // 2][:, t % 2, :],
+                func=ACT.Identity,
+                scale=vector_column(LN_COL_W, t),
+                bias=vector_column(LN_COL_B, t),
+            )
 
-        warm("vectors", 2)
+        warm("column3", 2)
         for t in range(PACK):
             nc.tensor.transpose(
                 out=prompt_t[:, t, :], in_=prompt_raw[:, t * P : (t + 1) * P], identity=ident_bf16[:]
             )
-        warm("vectors", 2)
+        warm("column3", 2)
         vectors_t = banks.tile([P, P], BF16, tag="vectors")
         nc.tensor.transpose(out=vectors_t[:], in_=vector_rows[:], identity=ident_bf16[:])
         partial_statistics(1)
@@ -267,19 +267,21 @@ def tile_tromptcell_pa_s_kernel(
                 nc.tensor.transpose(
                     out=prev_t[:, j, :], in_=prev_words[:, j * P : (j + 1) * P], identity=ident_f32[:]
                 )
-            warm("vectors", 1)
+            warm("column3", 1)
 
         reciprocal_std(3, ROW_TILES)
+        group_w_prompt(P, HALF)
         nc.scalar.copy(out=vectors[:], in_=vectors_t[:, 0 : VECTORS * PACK])
-        group_w_prompt(P, W_PROMPT_SPLIT)
+        group_w_prompt(HALF, W_PROMPT_SPLIT)
         for r in range(1, ROW_TILES):
             normalise(r)
         for t in range(PACK):
             nc.tensor.transpose(
                 out=prompt_z_t[:, t, :], in_=z[:, 0, t * P : (t + 1) * P], identity=ident_f32[:]
             )
+        warm("column3", 1)
         transpose_columns(1)
-        warm("vectors", 1)
+        warm("column3", 1)
         transpose_columns(2)
         transpose_prev()
         def copy_prev():
@@ -299,7 +301,7 @@ def tile_tromptcell_pa_s_kernel(
                 scale=vector_column(LN_PROMPT_W, t),
                 bias=vector_column(LN_PROMPT_B, t),
             )
-        warm("vectors", 1)
+        column_z_t = column_z_t + column_banks(1)
         transpose_columns(3)
         transpose_columns(4)
         warm("vectors", 1)
@@ -322,8 +324,8 @@ def tile_tromptcell_pa_s_kernel(
         for t in range(PACK):
             finish_columns(0, t)
         finish_columns(1, 0)
-        group_words(nc.vector.tensor_copy, col_grouped[:, P : HALF, :], col_planes[:, :, P : HALF])
-        group_words(nc.scalar.copy, col_grouped[:, 0 : P, :], col_planes[:, :, 0 : P])
+        group_words(nc.vector.tensor_copy, col_grouped[:, COL_SPLIT:HALF, :], col_planes[:, :, COL_SPLIT:HALF])
+        group_words(nc.scalar.copy, col_grouped[:, 0:COL_SPLIT, :], col_planes[:, :, 0:COL_SPLIT])
         for t in range(1, PACK):
             finish_columns(1, t)
 
@@ -409,21 +411,21 @@ def tile_tromptcell_pa_s_kernel(
         A, B, C = (0, 256), (256, 384), (384, 512)
         S, V = nc.scalar.copy, nc.vector.tensor_copy
         finish_x(0)
-        finish_x(1)
-        group_words(S, col_grouped[:, B[0] : B[1], :], col_planes[:, :, B[0] : B[1]])
         quantise_columns(*A)
         quantise_x(0)
         a0 = multiply(0, *A, "column0")
-        quantise_x(1)
-        a1 = multiply(1, *A, "column1")
-        group_words(V, col_grouped[:, C[0] : C[1], :], col_planes[:, :, C[0] : C[1]])
+        finish_x(1)
+        group_words(S, col_grouped[:, B[0] : B[1], :], col_planes[:, :, B[0] : B[1]])
+        group_words(S, col_grouped[:, C[0] : C[1], :], col_planes[:, :, C[0] : C[1]])
         store(S, a0, 0, *A)
         quantise_columns(*B)
-        b0, b1 = multiply(0, *B, "prev"), multiply(1, *B, "vectors")
+        b0 = multiply(0, *B, "prev")
+        quantise_x(1)
+        a1, b1 = multiply(1, *A, "column1"), multiply(1, *B, "vectors")
         quantise_columns(*C)
         c0, c1 = multiply(0, *C, "column2"), multiply(1, *C, "column3")
-        store(V, a1, 1, *A)
         store(S, b0, 0, *B)
-        store(V, b1, 1, *B)
-        store(S, c0, 0, *C)
+        store(V, a1, 1, *A)
+        store(S, b1, 1, *B)
         store(V, c1, 1, *C)
+        store(S, c0, 0, *C)

from contextlib import ExitStack

import concourse.mybir as mybir
from concourse.masks import make_identity

F32 = mybir.dt.float32
BF16 = mybir.dt.bfloat16
U32 = mybir.dt.uint32
U8 = mybir.dt.uint8
FP8X4 = mybir.dt.float8_e4m3fn_x4
ALU = mybir.AluOpType
ACT = mybir.ActivationFunctionType

P = 128
PACK = 4
D = P * PACK
SAMPLES = 2
COLUMNS = 512
COLUMN_TILES = COLUMNS // P
ROW_TILES = 1 + COLUMN_TILES
EPS = 1e-5
RUN = 4
HALF = 256
W_PROMPT_SPLIT = 352
W_PREV_SPLIT = 32
COL_SPLIT = 64

FLOPS = 2 * P * D * D + 2 * SAMPLES * P * D * D + 2 * SAMPLES * P * D * COLUMNS

LN_PROMPT_W = 0
LN_PROMPT_B = 1
B_IMP = 2
LN_COL_W = 3
LN_COL_B = 4
VECTORS = 5


def group_words(copy, grouped, planes):
    copy(
        out=grouped.rearrange("p (c i) t -> p c t i", i=RUN),
        in_=planes.rearrange("p t (c i) -> p c t i", i=RUN),
    )


def quantise(nc, codes, scales, grouped):
    nc.vector.quantize_mx(
        out=codes.bitcast(FP8X4),
        scales=scales,
        in_=grouped.rearrange("p c t -> p (c t)"),
    )


def tile_tromptcell_pa_s_kernel(
    tc,
    prev_cell_out,
    emb_prompt,
    ln_prompt_w,
    ln_prompt_b,
    W_imp,
    b_imp,
    emb_column,
    ln_col_w,
    ln_col_b,
    out,
):
    nc = tc.nc
    with ExitStack() as ctx:
        keep = ctx.enter_context(tc.tile_pool(name="keep", bufs=1))
        banks = ctx.enter_context(tc.psum_pool(name="banks", bufs=1))
        ctx.enter_context(tc.manual_schedule())

        vector_rows = keep.tile([P, P], BF16)
        vectors = keep.tile([P, VECTORS * PACK], F32)
        ident_bf16 = keep.tile([P, P], BF16)
        ident_f32 = keep.tile([P, P], F32)
        one = keep.tile([P, 1], F32)
        table_warmer = keep.tile([P, 1], F32)

        prompt_raw = keep.tile([P, D], BF16)
        column_raw = keep.tile([P, COLUMN_TILES, D], BF16)
        prev_raw = keep.tile([P, SAMPLES * D], BF16)
        w_prompt_raw = keep.tile([P, PACK, D], BF16)
        w_prev_raw = keep.tile([P, PACK, D], BF16)

        stats = keep.tile([P, ROW_TILES, 6], F32)
        mean_var = keep.tile([P, ROW_TILES, 2], F32)
        eps = keep.tile([P, 1], F32)
        row_sums = keep.tile([P, 2], F32)
        unused = keep.tile([P, D], BF16)
        rstd = keep.tile([P, ROW_TILES], F32)
        z = keep.tile([P, ROW_TILES, D], F32)

        residual = keep.tile([P, PACK, P], F32)
        pn_planes = keep.tile([P, PACK, P], BF16)
        col_planes = keep.tile([P, PACK, COLUMNS], BF16)

        def mx_operand(name, columns):
            grouped = keep.tile([P, columns, PACK], BF16, name=name + "_grouped", align_bytes=64)
            codes = keep.tile([P, columns], U32, name=name + "_codes", align_bytes=64)
            scales = keep.tile([P, columns], U8, name=name + "_scales", align_bytes=64)
            return grouped, codes, scales

        pn_grouped, pn_codes, pn_scales = mx_operand("pn", P)
        prev_grouped, prev_codes, prev_scales = mx_operand("prev", SAMPLES * P)
        w_prompt_grouped, w_prompt_codes, w_prompt_scales = mx_operand("w_prompt", D)
        w_prev_grouped, w_prev_codes, w_prev_scales = mx_operand("w_prev", D)
        col_grouped, col_codes, col_scales = mx_operand("col", COLUMNS)
        x_grouped, x_codes, x_scales = mx_operand("x", SAMPLES * P)

        nc.gpsimd.memset(vector_rows[:], 0.0)

        def load_vector(v, vector):
            nc.sync.dma_start(
                out=vector_rows[PACK * v : PACK * (v + 1), :],
                in_=vector.rearrange("(t p) -> t p", p=P),
            )

        column_view = emb_column.rearrange("(ct p) f -> p ct f", p=P)

        def load_columns(first, last):
            nc.sync.dma_start(
                out=column_raw[:, first:last, :], in_=column_view[:, first:last, :]
            )

        load_columns(0, 1)
        nc.sync.dma_start(out=prompt_raw[:], in_=emb_prompt)
        load_columns(1, 2)
        load_columns(2, COLUMN_TILES)
        nc.sync.dma_start(out=w_prompt_raw[:], in_=W_imp[0:D, :].rearrange("(t p) f -> p t f", p=P))
        load_vector(LN_PROMPT_W, ln_prompt_w)
        load_vector(LN_PROMPT_B, ln_prompt_b)
        load_vector(B_IMP, b_imp)
        load_vector(LN_COL_W, ln_col_w)
        load_vector(LN_COL_B, ln_col_b)
        nc.sync.dma_start(
            out=w_prev_raw[:].rearrange("p (u e) f -> p u e f", u=2),
            in_=W_imp[D : 2 * D, :].rearrange("(u p e) f -> p u e f", u=2, e=2),
        )
        nc.sync.dma_start(
            out=prev_raw[:].rearrange("p (n f) -> p n f", n=SAMPLES),
            in_=prev_cell_out.rearrange("n p f -> p n f"),
        )

        make_identity(nc, ident_bf16[:])
        make_identity(nc, ident_f32[:])
        nc.vector.memset(one[:], 1.0)
        nc.vector.tensor_scalar(out=eps[:], in0=one[:], scalar1=EPS, scalar2=None, op0=ALU.mult)
        nc.scalar.activation(out=table_warmer[:], in_=one[:], func=ACT.Abs_reciprocal_sqrt)

        row_tiles = [prompt_raw[:]] + [column_raw[:, ct, :] for ct in range(COLUMN_TILES)]

        def partial_statistics(r):
            nc.vector.bn_stats(out=stats[:, r, :], in_=row_tiles[r])

        def mean_and_variance(r):
            nc.vector.bn_aggr(out=mean_var[:, r, :], in_=stats[:, r, :])

        def reciprocal_std(first, last):
            nc.scalar.activation(
                out=rstd[:, first:last],
                in_=mean_var[:, first:last, 1],
                func=ACT.Abs_reciprocal_sqrt,
                bias=eps[:],
            )

        def normalise(r):
            nc.vector.tensor_scalar(
                out=z[:, r, :],
                in0=row_tiles[r],
                scalar1=mean_var[:, r, 0:1],
                scalar2=rstd[:, r : r + 1],
                op0=ALU.subtract,
                op1=ALU.mult,
            )

        def vector_column(v, t):
            return vectors[:, PACK * v + t : PACK * v + t + 1]


        nc.scalar.activation(
            out=unused[:],
            in_=prompt_raw[:],
            func=ACT.Identity,
            scale=-1.0,
            accum_out=row_sums[:, 0:1],
        )
        nc.scalar.activation(
            out=unused[:],
            in_=prompt_raw[:],
            func=ACT.Square,
            scale=float(D),
            bias=row_sums[:, 0:1],
            accum_out=row_sums[:, 1:2],
        )
        nc.scalar.activation(
            out=mean_var[:, 0, 0:1], in_=row_sums[:, 0:1], func=ACT.Copy, scale=-1.0 / D
        )
        nc.scalar.activation(
            out=rstd[:, 0:1],
            in_=row_sums[:, 1:2],
            func=ACT.Abs_reciprocal_sqrt,
            scale=1.0 / D**3,
            bias=eps[:],
        )

        def group_w_prompt(first, last):
            group_words(nc.scalar.copy, w_prompt_grouped[:, first:last, :], w_prompt_raw[:, :, first:last])

        def warm(tag, passes):
            unread = banks.tile([P, P], F32, tag=tag, name="unread_" + tag)
            for i in range(passes):
                nc.tensor.matmul(
                    out=unread[:], lhsT=ident_f32[:], rhs=ident_f32[:], start=True, stop=True
                )

        prompt_t = banks.tile([P, PACK, P], BF16, tag="prompt")
        prompt_z_t = banks.tile([P, PACK, P], F32, tag="prompt_z")
        prev_t = banks.tile([P, SAMPLES * 2, P], F32, tag="prev")
        def column_banks(half):
            return [
                banks.tile([P, 2, HALF], F32, tag="column%d" % i, name="column_z_t%d" % i)
                for i in (2 * half, 2 * half + 1)
            ]

        column_z_t = column_banks(0)

        def transpose_columns(r):
            half, first = divmod((r - 1) * P, HALF)
            for t in range(PACK):
                nc.tensor.transpose(
                    out=column_z_t[2 * half + t // 2][:, t % 2, first : first + P],
                    in_=z[:, r, t * P : (t + 1) * P],
                    identity=ident_f32[:],
                )

        def finish_columns(half, t):
            nc.scalar.activation(
                out=col_planes[:, t, half * HALF : (half + 1) * HALF],
                in_=column_z_t[2 * half + t // 2][:, t % 2, :],
                func=ACT.Identity,
                scale=vector_column(LN_COL_W, t),
                bias=vector_column(LN_COL_B, t),
            )

        warm("column3", 2)
        for t in range(PACK):
            nc.tensor.transpose(
                out=prompt_t[:, t, :], in_=prompt_raw[:, t * P : (t + 1) * P], identity=ident_bf16[:]
            )
        warm("column3", 2)
        vectors_t = banks.tile([P, P], BF16, tag="vectors")
        nc.tensor.transpose(out=vectors_t[:], in_=vector_rows[:], identity=ident_bf16[:])
        partial_statistics(1)
        partial_statistics(2)
        mean_and_variance(1)
        partial_statistics(3)
        mean_and_variance(2)
        partial_statistics(4)
        mean_and_variance(3)
        reciprocal_std(1, 3)
        group_w_prompt(0, P)
        normalise(0)
        mean_and_variance(4)
        def transpose_prev():
            prev_words = prev_raw[:].bitcast(F32)
            for j in range(SAMPLES * 2):
                nc.tensor.transpose(
                    out=prev_t[:, j, :], in_=prev_words[:, j * P : (j + 1) * P], identity=ident_f32[:]
                )
            warm("column3", 1)

        reciprocal_std(3, ROW_TILES)
        group_w_prompt(P, HALF)
        nc.scalar.copy(out=vectors[:], in_=vectors_t[:, 0 : VECTORS * PACK])
        group_w_prompt(HALF, W_PROMPT_SPLIT)
        for r in range(1, ROW_TILES):
            normalise(r)
        for t in range(PACK):
            nc.tensor.transpose(
                out=prompt_z_t[:, t, :], in_=z[:, 0, t * P : (t + 1) * P], identity=ident_f32[:]
            )
        warm("column3", 1)
        transpose_columns(1)
        warm("column3", 1)
        transpose_columns(2)
        transpose_prev()
        def copy_prev():
            nc.scalar.copy(
                out=prev_grouped[:]
                .rearrange("p c t -> p (c t)")
                .bitcast(F32)
                .rearrange("p (n w u) -> p n w u", n=SAMPLES, u=2),
                in_=prev_t[:].rearrange("p (n u) w -> p n w u", u=2),
            )

        for t in range(PACK):
            nc.scalar.activation(
                out=pn_planes[:, t, :],
                in_=prompt_z_t[:, t, :],
                func=ACT.Identity,
                scale=vector_column(LN_PROMPT_W, t),
                bias=vector_column(LN_PROMPT_B, t),
            )
        column_z_t = column_z_t + column_banks(1)
        transpose_columns(3)
        transpose_columns(4)
        warm("vectors", 1)
        group_words(nc.scalar.copy, w_prev_grouped[:, 0:W_PREV_SPLIT, :], w_prev_raw[:, :, 0:W_PREV_SPLIT])
        group_words(nc.scalar.copy, pn_grouped[:], pn_planes[:])
        copy_prev()
        group_words(nc.vector.tensor_copy, w_prompt_grouped[:, W_PROMPT_SPLIT:, :], w_prompt_raw[:, :, W_PROMPT_SPLIT:])
        group_words(nc.vector.tensor_copy, w_prev_grouped[:, W_PREV_SPLIT:, :], w_prev_raw[:, :, W_PREV_SPLIT:])
        quantise(nc, w_prompt_codes[:], w_prompt_scales[:], w_prompt_grouped[:])
        quantise(nc, w_prev_codes[:], w_prev_scales[:], w_prev_grouped[:])
        quantise(nc, pn_codes[:], pn_scales[:], pn_grouped[:])
        quantise(nc, prev_codes[:], prev_scales[:], prev_grouped[:])

        nc.vector.tensor_tensor(
            out=residual[:],
            in0=prompt_t[:],
            in1=vectors[:, PACK * B_IMP : PACK * (B_IMP + 1)].unsqueeze(2).to_broadcast([P, PACK, P]),
            op=ALU.add,
        )
        for t in range(PACK):
            finish_columns(0, t)
        finish_columns(1, 0)
        group_words(nc.vector.tensor_copy, col_grouped[:, COL_SPLIT:HALF, :], col_planes[:, :, COL_SPLIT:HALF])
        group_words(nc.scalar.copy, col_grouped[:, 0:COL_SPLIT, :], col_planes[:, :, 0:COL_SPLIT])
        for t in range(1, PACK):
            finish_columns(1, t)

        def warm_mx(tag, passes):
            unread = banks.tile([P, D], F32, tag=tag, name="unread_mx_" + tag)
            for i in range(passes):
                nc.tensor.matmul_mx(
                    out=unread[:],
                    lhsT=w_prompt_codes[:, 0:P].bitcast(FP8X4),
                    lhsT_scale=w_prompt_scales[:, 0:P],
                    rhs=w_prompt_codes[:].bitcast(FP8X4),
                    rhs_scale=w_prompt_scales[:],
                    start=True,
                    stop=True,
                )

        warm_mx("prev", 2)
        x_t = [
            banks.tile([P, PACK, P], F32, tag=tag, name="x_t%d" % n)
            for n, tag in enumerate(("vectors", "prompt_z"))
        ]
        for n in range(SAMPLES):
            prompts = slice(n * P, (n + 1) * P)
            for t in range(PACK):
                features = slice(t * P, (t + 1) * P)
                nc.tensor.matmul_mx(
                    out=x_t[n][:, t, :],
                    lhsT=w_prompt_codes[:, features].bitcast(FP8X4),
                    lhsT_scale=w_prompt_scales[:, features],
                    rhs=pn_codes[:].bitcast(FP8X4),
                    rhs_scale=pn_scales[:],
                    start=True,
                    stop=False,
                )
                nc.tensor.matmul_mx(
                    out=x_t[n][:, t, :],
                    lhsT=w_prev_codes[:, features].bitcast(FP8X4),
                    lhsT_scale=w_prev_scales[:, features],
                    rhs=prev_codes[:, prompts].bitcast(FP8X4),
                    rhs_scale=prev_scales[:, prompts],
                    start=False,
                    stop=True,
                )

        warm_mx("prompt", 3)

        def finish_x(n):
            nc.vector.tensor_tensor(
                out=x_grouped[:, n * P : (n + 1) * P, :].rearrange("p (c i) t -> p c t i", i=RUN),
                in0=x_t[n][:].rearrange("p t (c i) -> p c t i", i=RUN),
                in1=residual[:].rearrange("p t (c i) -> p c t i", i=RUN),
                op=ALU.add,
            )

        def quantise_columns(first, last):
            columns = slice(first, last)
            quantise(nc, col_codes[:, columns], col_scales[:, columns], col_grouped[:, columns, :])

        def quantise_x(n):
            prompts = slice(n * P, (n + 1) * P)
            quantise(nc, x_codes[:, prompts], x_scales[:, prompts], x_grouped[:, prompts, :])

        def multiply(n, first, last, tag):
            prompts = slice(n * P, (n + 1) * P)
            columns = slice(first, last)
            scores = banks.tile([P, last - first], F32, tag=tag, name="scores%d_%d" % (n, first))
            nc.tensor.matmul_mx(
                out=scores[:],
                lhsT=x_codes[:, prompts].bitcast(FP8X4),
                lhsT_scale=x_scales[:, prompts],
                rhs=col_codes[:, columns].bitcast(FP8X4),
                rhs_scale=col_scales[:, columns],
                start=True,
                stop=True,
            )
            return scores

        def store(copy, scores, n, first, last):
            scores_sb = keep.tile([P, last - first], F32, name="scores_sb%d_%d" % (n, first))
            copy(out=scores_sb[:], in_=scores[:])
            nc.sync.dma_start(out=out[n, :, first:last], in_=scores_sb[:])

        A, B, C = (0, 256), (256, 384), (384, 512)
        S, V = nc.scalar.copy, nc.vector.tensor_copy
        finish_x(0)
        quantise_columns(*A)
        quantise_x(0)
        a0 = multiply(0, *A, "column0")
        finish_x(1)
        group_words(S, col_grouped[:, B[0] : B[1], :], col_planes[:, :, B[0] : B[1]])
        group_words(S, col_grouped[:, C[0] : C[1], :], col_planes[:, :, C[0] : C[1]])
        store(S, a0, 0, *A)
        quantise_columns(*B)
        b0 = multiply(0, *B, "prev")
        quantise_x(1)
        a1, b1 = multiply(1, *A, "column1"), multiply(1, *B, "vectors")
        quantise_columns(*C)
        c0, c1 = multiply(0, *C, "column2"), multiply(1, *C, "column3")
        store(S, b0, 0, *B)
        store(V, a1, 1, *A)
        store(S, b1, 1, *B)
        store(V, c1, 1, *C)
        store(S, c0, 0, *C)
